import numpy as np
import ml_dtypes


def mxq(x, axis, fmt="e4m3"):
    dtype, down = {"e4m3": (ml_dtypes.float8_e4m3fn, 7), "e5m2": (ml_dtypes.float8_e5m2, 14)}[fmt]
    v = np.moveaxis(np.asarray(x, np.float32).astype(ml_dtypes.bfloat16).astype(np.float64), axis, -1)
    blocks = v.reshape(v.shape[:-1] + (-1, 32))
    amax = np.abs(blocks).max(-1, keepdims=True)
    byte = np.maximum(np.where(amax > 0, np.frexp(amax)[1] - 1 + 127, 0) - down, 1)
    scale = np.exp2(byte - 127.0)
    codes = (blocks / scale).astype(np.float32).astype(dtype).astype(np.float64)
    return np.moveaxis((codes * scale).reshape(v.shape), -1, axis)


WIDE = False


def mx_kscale(k):
    if not WIDE:
        return np.ones(k)
    levels = np.array([10, -10, 5, -5, 0])
    if k % 512:
        return np.exp2(np.random.permutation(np.resize(levels, k // 32))).repeat(32)
    a = np.empty((k // 512, 16))
    for p in range(k // 512):
        a[p, :8] = np.random.permutation(np.resize(levels, 8))
        for g in range(8):
            far = levels[np.abs(levels - a[p, g]) >= 10]
            a[p, g + 8] = far[np.random.randint(len(far))]
    return np.exp2(a.ravel()).repeat(32)


BF16 = ml_dtypes.bfloat16


def bf(x):
    return np.asarray(x, np.float32).astype(BF16)


def f64(x):
    return np.asarray(x).astype(np.float64)


B, H, FEAT, AUX, NS, FC, C = 1024, 1024, 128, 128, 2, 1024, 256
IN = FEAT + AUX + NS


def sigmoid(v):
    return 1.0 / (1.0 + np.exp(-v))


def setup_inputs():
    s = mx_kscale(H)
    s = s / s.max()
    col = np.concatenate([np.full(FEAT, 0.6 / np.sqrt(FEAT)), np.full(AUX, 0.6 / np.sqrt(AUX)), np.full(NS, 0.6 / np.sqrt(NS))])
    return {"x": bf(np.random.standard_normal((B, NS))),
            "feat": bf(np.random.standard_normal((B, FEAT))),
            "aux1": bf(np.random.standard_normal((B, AUX))),
            "h": bf(np.random.standard_normal((B, H)) * s),
            "w_ih": bf(np.random.standard_normal((3 * H, IN)) * col),
            "w_hh": bf(np.random.standard_normal((3 * H, H)) / np.sqrt(H) / s),
            "b_ih": bf(np.random.standard_normal(3 * H) * 0.3),
            "b_hh": bf(np.random.standard_normal(3 * H) * 0.3)}


def reference(x, feat, aux1, h, w_ih, w_hh, b_ih, b_hh):
    hh, wi, xx = f64(h), f64(w_ih), f64(x)
    gi = f64(feat) @ wi[:, :FEAT].T + f64(aux1) @ wi[:, FEAT:FEAT + AUX].T
    for j in range(NS):
        gi = gi + xx[:, j:j + 1] * wi[:, FEAT + AUX + j][None, :]
    gi = gi + f64(b_ih)
    gh = (mxq(hh, 1, "e4m3") @ mxq(f64(w_hh), 1, "e4m3").T) + f64(b_hh)
    i_r, i_z, i_n = np.split(gi, 3, axis=1)
    h_r, h_z, h_n = np.split(gh, 3, axis=1)
    r = sigmoid(i_r + h_r)
    z = sigmoid(i_z + h_z)
    n = np.tanh(i_n + r * h_n)
    return (1.0 - z) * n + z * hh

@@ -1,0 +1,451 @@
+from contextlib import ExitStack
+
+import concourse.mybir as mybir
+from concourse.masks import make_identity
+
+F32 = mybir.dt.float32
+BF16 = mybir.dt.bfloat16
+U32 = mybir.dt.uint32
+U8 = mybir.dt.uint8
+FP8X4 = mybir.dt.float8_e4m3fn_x4
+ALU = mybir.AluOpType
+AF = mybir.ActivationFunctionType
+
+P = 128
+B = 1024
+H = 1024
+IN = 258
+NB = 512
+NSLOT = 16
+O_AT = {8: [(0, 0)], 9: [(0, 1)], 10: [(0, 2)], 11: [(0, 3), (0, 4)], 12: [(0, 5)], 13: [(0, 6), (0, 7)],
+        15: [(1, 0), (1, 1)], 16: [(1, 2), (1, 3)], 17: [(1, 4), (1, 5), (1, 6), (1, 7)]}
+PD = 2
+LASTP = NSLOT // 2 - 1
+FLOPS = 2 * B * 3 * H * (H + IN)
+
+
+def weave(ms, ts, late):
+    gaps = len(ms) - 1
+    total = len(ts) + len(late)
+    first = list(ts)
+    second = list(late)
+    done = 0
+    for i, m in enumerate(ms):
+        m()
+        if i < gaps:
+            hi = ((i + 1) * total + gaps - 1) // gaps
+            while done < hi:
+                if i >= 3 and len(second) > 0:
+                    second.pop(0)()
+                elif len(first) > 0:
+                    first.pop(0)()
+                else:
+                    break
+                done += 1
+
+
+def tile_wavernncell_pa_kernel(tc, x, feat, aux1, h, w_ih, w_hh, b_ih, b_hh, out):
+    nc = tc.nc
+    with ExitStack() as ctx:
+        ctx.enter_context(tc.manual_schedule())
+        const = ctx.enter_context(tc.tile_pool(name="const", bufs=1))
+        wpool = ctx.enter_context(tc.tile_pool(name="wpool", bufs=2))
+        work = ctx.enter_context(tc.tile_pool(name="work", bufs=2))
+        acc = ctx.enter_context(tc.psum_pool(name="acc", bufs=5))
+        tp = ctx.enter_context(tc.psum_pool(name="tp", bufs=3))
+
+        feat_v = feat.rearrange("(t p) k -> p t k", p=P)
+        aux_v = aux1.rearrange("(t p) k -> p t k", p=P)
+        x_v = x.rearrange("(t p) c -> p t c", p=P)
+        h_v = h.rearrange("(t p) k -> p t k", p=P)
+        out_v = out.rearrange("(t p) j -> p t j", p=P)
+        wih_v = w_ih.rearrange("(G g q d e) k -> g d q G (e k)", G=3, g=2, q=P, d=2, e=2)
+        whh_v = w_hh.rearrange("(G g q d e) k -> g d q G (e k)", G=3, g=2, q=P, d=2, e=2)
+        bih_v = b_ih.rearrange("(m q f) -> q m f", m=6, q=P, f=4)
+        bhh_v = b_hh.rearrange("(m q f) -> q m f", m=6, q=P, f=4)
+
+        ident_f = const.tile([P, P], F32, name="ident_f")
+        ident_b = const.tile([P, P], BF16, name="ident_b")
+        warm = const.tile([P, 1], F32, name="warm")
+        fn = const.tile([P, 8, P], BF16, name="fn")
+        an = const.tile([P, 8, P], BF16, name="an")
+        xn = const.tile([P, 8, P], BF16, name="xn")
+        feat_t = const.tile([P, B], BF16, name="feat_t")
+        aux_t = const.tile([P, B], BF16, name="aux_t")
+        x_t = const.tile([P, B], BF16, name="x_t")
+        xb = const.tile([P, 2 * B], BF16, name="xb")
+        hn = const.tile([P, 8, H], BF16, name="hn")
+        hg = const.tile([P, 2, B, 4], BF16, name="hg", align_bytes=64)
+        hc = const.tile([P, 2, B], U32, name="hc", align_bytes=64)
+        hs = const.tile([P, 2, B], U8, name="hs", align_bytes=64)
+        wx = const.tile([P, 4, 3, P], BF16, name="wx")
+        bi = const.tile([P, 12, 2], BF16, name="bi")
+        bh2 = const.tile([P, 12, 2], BF16, name="bh2")
+        b_r = const.tile([P, 4, 2], F32, name="b_r")
+        b_zn = const.tile([P, 4, 2], F32, name="b_zn")
+        b_in = const.tile([P, 4, 2], F32, name="b_in")
+        b_hn = const.tile([P, 4, 2], F32, name="b_hn")
+
+        wt = {}
+        ut = {}
+        pr = {}
+        ft = {}
+        ra = {}
+
+        def load_w(c):
+            win = wpool.tile([P, 3, 2 * IN], BF16, name="win", tag="win")
+            wn = wpool.tile([P, 3, 2 * H], BF16, name="wn", tag="wn")
+            if c == 0:
+                nc.sync.dma_start(out=win[:], in_=wih_v[c // 2, c % 2])
+            for G in range(3):
+                nc.sync.dma_start(out=wn[:, G, :], in_=whh_v[c // 2, c % 2, :, G, :])
+            if c > 0:
+                nc.sync.dma_start(out=win[:], in_=wih_v[c // 2, c % 2])
+            wt[c] = {"win": win, "wn": wn}
+
+        nc.vector.memset(warm[:], 0.0)
+        nc.vector.memset(xn[:], 0.0)
+        nc.vector.memset(wx[:], 0.0)
+        make_identity(nc, ident_b[:])
+        make_identity(nc, ident_f[:])
+        nc.sync.dma_start(out=fn[:], in_=feat_v)
+        nc.sync.dma_start(out=an[:], in_=aux_v)
+        with nc.allow_non_contiguous_dma(reason="small vectors, four bytes a piece"):
+            nc.scalar.dma_start(out=xn[:, :, 0:2], in_=x_v)
+            nc.scalar.dma_start(out=bi[:].rearrange("p (m d) e -> p m (d e)", d=2), in_=bih_v)
+            nc.scalar.dma_start(out=bh2[:].rearrange("p (m d) e -> p m (d e)", d=2), in_=bhh_v)
+        nc.scalar.dma_start(out=xb[:], in_=x.rearrange("b c -> (b c)").partition_broadcast(P))
+        nc.scalar.activation(out=warm[:], in_=warm[:], func=AF.Sigmoid)
+        win0 = wpool.tile([P, 3, 2 * IN], BF16, name="win", tag="win")
+        nc.sync.dma_start(out=win0[:], in_=wih_v[0, 0])
+        for k in range(2):
+            nc.sync.dma_start(out=hn[:, 2 * k:2 * k + 2, :], in_=h_v[:, 2 * k:2 * k + 2, :])
+        wn0 = wpool.tile([P, 3, 2 * H], BF16, name="wn", tag="wn")
+        for G in range(3):
+            nc.sync.dma_start(out=wn0[:, G, :], in_=whh_v[0, 0, :, G, :])
+        for k in range(2, 4):
+            nc.sync.dma_start(out=hn[:, 2 * k:2 * k + 2, :], in_=h_v[:, 2 * k:2 * k + 2, :])
+        wt[0] = {"win": win0, "wn": wn0}
+        load_w(1)
+
+        xb_v = xb[:].rearrange("p (b c) -> p b c", c=2)
+        hn_w = hn[:].bitcast(F32)
+        hg_w = hg[:].bitcast(F32)
+
+        def copy_on(eng, dst, src):
+            if eng == "act":
+                nc.scalar.copy(out=dst, in_=src)
+            else:
+                nc.vector.tensor_copy(out=dst, in_=src)
+
+        def tr(dst, src, ident):
+            return lambda: nc.tensor.transpose(dst, src, ident[:])
+
+        def job_rows(src, dst):
+            pt = tp.tile([P, 8, P], BF16, name="pt_f", tag="tp")
+            ts = [tr(pt[:, t, :], src[:, t, :], ident_b) for t in range(8)]
+            return ts, lambda eng: copy_on(eng, dst[:], pt[:].rearrange("p t b -> p (t b)"))
+
+        def job_h(t):
+            pt = tp.tile([P, 4, P], F32, name="pt_h", tag="tp")
+            ts = [tr(pt[:, wb, :], hn_w[:, t, 256 * (wb // 2) + wb % 2:256 * (wb // 2 + 1):2], ident_f) for wb in range(4)]
+            return ts, lambda eng: copy_on(eng, hg_w[:, :, t * P:(t + 1) * P, :],
+                                           pt[:].rearrange("p (g u) b -> p g b u", g=2))
+
+        def begin_w(c):
+            w = wt[c]
+            w["w01"] = wpool.tile([P, 3, 2, 2], F32, name="w01", tag="w01")
+            w["wit"] = wpool.tile([P, 15, P], BF16, name="wit", tag="wit")
+            w["wg"] = wpool.tile([P, 6, 2, P, 4], BF16, name="wg", tag="wg", align_bytes=64)
+            w["wc"] = wpool.tile([P, 6, 2, P], U32, name="wc", tag="wc", align_bytes=64)
+            w["ws"] = wpool.tile([P, 6, 2, P], U8, name="ws", tag="ws", align_bytes=64)
+
+        def small_w(c):
+            win_v = wt[c]["win"][:].rearrange("p G (e k) -> p G e k", e=2)
+            nc.scalar.copy(out=wt[c]["w01"][:], in_=win_v[:, :, :, 256:258])
+            nc.scalar.copy(out=wx[:, c, 0:2, 0:2], in_=win_v[:, 0, :, 256:258])
+            nc.scalar.copy(out=wx[:, c, 2, 0:2], in_=win_v[:, 2, 0, 256:258])
+
+        def job_ia(c):
+            win_v = wt[c]["win"][:].rearrange("p G (e k) -> p G e k", e=2)
+            wit = wt[c]["wit"]
+            pt = tp.tile([P, 8, P], BF16, name="pt_a", tag="tp")
+            ts = [tr(pt[:, i, :], win_v[:, i // 4, (i // 2) % 2, (i % 2) * P:(i % 2 + 1) * P], ident_b)
+                  for i in range(8)]
+            return ts, lambda eng: copy_on(eng, wit[:, 0:8, :], pt[:])
+
+        def job_ib(c):
+            win_v = wt[c]["win"][:].rearrange("p G (e k) -> p G e k", e=2)
+            wit = wt[c]["wit"]
+            pt = tp.tile([P, 8, P], BF16, name="pt_b", tag="tp")
+            ts = [tr(pt[:, i, :], win_v[:, 2, i // 2, (i % 2) * P:(i % 2 + 1) * P], ident_b) for i in range(4)]
+            ts.extend([tr(pt[:, 4 + i, :], wx[:, c, i, :], ident_b) for i in range(3)])
+            return ts, lambda eng: copy_on(eng, wit[:, 8:15, :], pt[:, 0:7, :])
+
+        def job_w(c, ge):
+            wn_w = wt[c]["wn"][:].bitcast(F32)
+            wg_w = wt[c]["wg"][:].bitcast(F32)
+            G, e = ge // 2, ge % 2
+            pt = tp.tile([P, 4, P], F32, name="pt_w", tag="tp")
+            ts = [tr(pt[:, wb, :], wn_w[:, G, e * 512 + 256 * (wb // 2) + wb % 2:e * 512 + 256 * (wb // 2 + 1):2], ident_f)
+                  for wb in range(4)]
+            return ts, lambda eng: copy_on(eng, wg_w[:, ge, :, :, :],
+                                           pt[:].rearrange("p (g u) q -> p g q u", g=2))
+
+        def quant_w(c, G):
+            w = wt[c]
+            nc.vector.quantize_mx(
+                out=w["wc"][:, 2 * G:2 * G + 2, :, :].rearrange("p a g q -> p (a g q)").bitcast(FP8X4),
+                scales=w["ws"][:, 2 * G:2 * G + 2, :, :].rearrange("p a g q -> p (a g q)"),
+                in_=w["wg"][:, 2 * G:2 * G + 2, :, :, :].rearrange("p a g q t -> p (a g q t)"))
+
+        def quant_h(g, bh):
+            bs = slice(bh * NB, (bh + 1) * NB)
+            nc.vector.quantize_mx(out=hc[:, g, bs].bitcast(FP8X4), scales=hs[:, g, bs],
+                                  in_=hg[:, g, bs, :].rearrange("p b t -> p (b t)"))
+
+        def job_o(g, t):
+            js = slice(512 * g, 512 * (g + 1))
+            pt = tp.tile([P, 4, P], F32, name="pt_o", tag="tp")
+            ts = [tr(pt[:, 2 * d + e, :], ft[2 * g + d][:, e, t * P:(t + 1) * P], ident_f)
+                  for d in range(2) for e in range(2)]
+
+            def ev(eng):
+                o_t = work.tile([P, 512], F32, name="o_t", tag="o_t", bufs=4)
+                nc.vector.tensor_tensor(out=o_t[:].rearrange("p (q f) -> p q f", f=4),
+                                        in0=pt[:].rearrange("p f q -> p q f"),
+                                        in1=hn[:, t, js].rearrange("p (q f) -> p q f", f=4),
+                                        op=ALU.add)
+                nc.sync.dma_start(out=out_v[:, t, js], in_=o_t[:])
+            return ts, ev
+
+        def run_job(job, eng):
+            for t in job[0]:
+                t()
+            job[1](eng)
+
+        begin_w(0)
+        run_job(job_rows(fn, feat_t), "act")
+        run_job(job_rows(an, aux_t), "dve")
+        small_w(0)
+        run_job(job_ia(0), "act")
+        run_job(job_ib(0), "dve")
+        run_job(job_rows(xn, x_t), "act")
+        for t in range(4):
+            run_job(job_h(t), "act" if t % 2 == 0 else "dve")
+        for ge in range(6):
+            run_job(job_w(0, ge), "act" if ge % 2 == 0 else "dve")
+            if ge == 0:
+                quant_h(0, 0)
+                quant_h(1, 0)
+            if ge == 3:
+                quant_w(0, 0)
+            if ge == 5:
+                quant_w(0, 1)
+        quant_w(0, 2)
+        nc.vector.tensor_tensor(out=b_r[:], in0=bi[:, 0:4, :], in1=bh2[:, 0:4, :], op=ALU.add)
+        nc.vector.scalar_tensor_tensor(out=b_zn[:], in0=bi[:, 4:8, :], scalar=-1.0, in1=bh2[:, 4:8, :],
+                                       op0=ALU.mult, op1=ALU.subtract)
+        nc.vector.tensor_copy(out=b_in[:], in_=bi[:, 8:12, :])
+        nc.vector.tensor_copy(out=b_hn[:], in_=bh2[:, 8:12, :])
+
+
+        def unit_of(s):
+            return s // 4, (s // 2) % 2, s % 2
+
+        def mm(ps, lhsT, rhs, start, stop):
+            return lambda: nc.tensor.matmul(ps[:], lhsT=lhsT, rhs=rhs, start=start, stop=stop)
+
+        def tacc(dst, src, stop):
+            return lambda: nc.tensor.matmul(dst, lhsT=src, rhs=ident_f[:], is_transpose=True, start=False, stop=stop)
+
+        def pe_ra(s):
+            c, bh, e = unit_of(s)
+            wc, ws = wt[c]["wc"], wt[c]["ws"]
+            ps = acc.tile([P, 4, P], F32, name="gra", tag="acc")
+            for i in range(4):
+                cs = slice(bh * NB + i * P, bh * NB + (i + 1) * P)
+                for kg in range(2):
+                    nc.tensor.matmul_mx(ps[:, i, :], lhsT=hc[:, kg, cs].bitcast(FP8X4), lhsT_scale=hs[:, kg, cs],
+                                        rhs=wc[:, e, kg, :].bitcast(FP8X4), rhs_scale=ws[:, e, kg, :],
+                                        start=(kg == 0), stop=(kg == 1))
+            ra[s] = work.tile([P, 4, P], F32, name="grs", tag="grs", bufs=2)
+            return lambda: nc.scalar.copy(out=ra[s][:], in_=ps[:])
+
+        def pe_unit(s, ts):
+            c, bh, e = unit_of(s)
+            w = wt[c]
+            wit, wc, ws = w["wit"], w["wc"], w["ws"]
+            bs = slice(bh * NB, (bh + 1) * NB)
+            gi_r = acc.tile([P, NB], F32, name="gi_r", tag="acc")
+            gi_z = acc.tile([P, NB], F32, name="gi_z", tag="acc")
+            gi_n = acc.tile([P, NB], F32, name="gi_n", tag="acc")
+            ms = [mm(gi_r, wit[:, 2 * e, :], feat_t[:, bs], True, False),
+                  mm(gi_r, wit[:, 2 * e + 1, :], aux_t[:, bs], False, False),
+                  mm(gi_r, wit[:, 12 + e, :], x_t[:, bs], False, False),
+                  mm(gi_z, wit[:, 4 + 2 * e, :], feat_t[:, bs], True, False),
+                  mm(gi_z, wit[:, 4 + 2 * e + 1, :], aux_t[:, bs], False, True),
+                  mm(gi_n, wit[:, 8 + 2 * e, :], feat_t[:, bs], True, False),
+                  mm(gi_n, wit[:, 8 + 2 * e + 1, :], aux_t[:, bs], False, e == 1)]
+            if e == 0:
+                ms.append(mm(gi_n, wit[:, 14, :], x_t[:, bs], False, True))
+            grs = ra[s]
+            late = [tacc(gi_r[:, i * P:(i + 1) * P], grs[:, i, :], i == 3) for i in range(4)]
+            weave(ms, ts, late)
+            gh = {}
+            for G in (2, 1):
+                ps = acc.tile([P, NB], F32, name="gh%d" % G, tag="acc")
+                for kg in range(2):
+                    nc.tensor.matmul_mx(ps[:], lhsT=wc[:, 2 * G + e, kg, :].bitcast(FP8X4),
+                                        lhsT_scale=ws[:, 2 * G + e, kg, :],
+                                        rhs=hc[:, kg, bs].bitcast(FP8X4), rhs_scale=hs[:, kg, bs],
+                                        start=(kg == 0), stop=(kg == 1))
+                gh[G] = ps
+            ra_out = pe_ra(s + 1) if s + 1 < NSLOT else None
+            if e == 0:
+                pr[s // 2] = {"un": work.tile([P, 2, NB], F32, name="un", tag="un", bufs=4),
+                              "uz": work.tile([P, 2, NB], F32, name="uz", tag="uz", bufs=4),
+                              "vz": work.tile([P, 2, NB], F32, name="vz", tag="vz", bufs=2)}
+            ut[s] = {"ra_out": ra_out, "gi_r": gi_r, "gi_n": gi_n, "gi_z": gi_z, "gh": gh,
+                     "ar": work.tile([P, NB], F32, name="ar", tag="ar", bufs=2),
+                     "qn": work.tile([P, NB], F32, name="qn", tag="qn", bufs=3)}
+
+        def stt(dst, in0, scalar, in1, op0, op1):
+            nc.vector.scalar_tensor_tensor(out=dst, in0=in0, scalar=scalar, in1=in1, op0=op0, op1=op1)
+
+        def tt(eng, dst, in0, in1, op):
+            if eng == "dve":
+                nc.vector.tensor_tensor(out=dst, in0=in0, in1=in1, op=op)
+            else:
+                nc.gpsimd.tensor_tensor(out=dst, in0=in0, in1=in1, op=op)
+
+        def h_t(p, i):
+            c, bh = p // 2, p % 2
+            return hg[:, c // 2, bh * NB:(bh + 1) * NB, 2 * (c % 2) + i]
+
+        def sub_h(eng, p, lo, hi):
+            un = pr[p]["un"]
+            for i in range(lo, hi):
+                tt(eng, un[:, i, :], un[:, i, :], h_t(p, i), ALU.subtract)
+
+        def mul_z(eng, p, lo, hi):
+            c, bh = p // 2, p % 2
+            if c not in ft:
+                ft[c] = work.tile([P, 2, B], F32, name="f_t", tag="f_t", bufs=4)
+            for i in range(lo, hi):
+                tt(eng, ft[c][:, i, bh * NB:(bh + 1) * NB], pr[p]["uz"][:, i, :], pr[p]["un"][:, i, :], ALU.mult)
+
+        def prep_jobs(s):
+            c, k = s // 4 + 1, s % 4
+            if c > 3:
+                return []
+            seq = [("w", c, ge) for ge in range(6)] + [("ia", c, 0), ("ib", c, 0)]
+            cuts = (0, 0, 3, 6, 8) if c == 1 else (0, 2, 4, 6, 8)
+            return seq[cuts[k]:cuts[k + 1]]
+
+        def make_job(d):
+            if d[0] == "w":
+                if d[2] == 0:
+                    begin_w(d[1])
+                return job_w(d[1], d[2])
+            if d[0] == "ia":
+                return job_ia(d[1])
+            if d[0] == "ib":
+                return job_ib(d[1])
+            return job_o(d[1], d[2])
+
+        def slot(s):
+            c, bh, e = unit_of(s)
+            k = s % 4
+            p = s // 2
+            main = s < NSLOT
+            if main and k == 0 and c + 2 < 4:
+                load_w(c + 2)
+            jobs = [make_job(d) for d in prep_jobs(s)] if main else []
+            ojobs = [job_o(co, io) for co, io in O_AT.get(s, [])]
+            ts = []
+            for j in jobs + ojobs:
+                ts.extend(j[0])
+            if main:
+                pe_unit(s, ts)
+                u = ut[s]
+                pp = pr[p]
+                w01 = wt[c]["w01"]
+                bs = slice(bh * NB, (bh + 1) * NB)
+                x0 = xb_v[:, bs, 0]
+                x1 = xb_v[:, bs, 1]
+                un = pp["un"][:, e, :]
+                uz = pp["uz"][:, e, :]
+                vz = pp["vz"][:, e, :]
+                ar = u["ar"]
+                nc.scalar.activation(out=ar[:], in_=u["gi_r"][:], func=AF.Sigmoid, bias=b_r[:, c, e:e + 1], scale=1.0)
+                for j in jobs:
+                    j[1]("act")
+                if u["ra_out"] is not None:
+                    u["ra_out"]()
+                if c + 1 < 4 and k == 2:
+                    small_w(c + 1)
+                for d in prep_jobs(s - 1) if s > 0 else []:
+                    if d[0] == "w" and d[2] % 2 == 1:
+                        quant_w(d[1], d[2] // 2)
+                stt(uz, x0, w01[:, 1, e, 0:1], u["gi_z"][:], ALU.mult, ALU.add)
+                if e == 1:
+                    stt(un, x0, w01[:, 2, e, 0:1], u["gi_n"][:], ALU.mult, ALU.add)
+                if e == 1:
+                    stt(un, x1, w01[:, 2, e, 1:2], un, ALU.mult, ALU.add)
+                stt(u["qn"][:], u["gh"][2][:], b_hn[:, c, e:e + 1], ar[:], ALU.add, ALU.mult)
+                if e == 0:
+                    tt("dve", un, u["gi_n"][:], u["qn"][:], ALU.add)
+                stt(vz, x1, w01[:, 1, e, 1:2], u["gh"][1][:], ALU.mult, ALU.add)
+                for j in ojobs:
+                    j[1]("dve")
+                if p >= PD:
+                    if e == 1:
+                        tt("dve", un, un, u["qn"][:], ALU.add)
+                    tt("dve", uz, uz, vz, ALU.add)
+            else:
+                for t in ts:
+                    t()
+                for j in ojobs:
+                    j[1]("dve")
+            if 1 <= s <= NSLOT:
+                tanh_of(s - 1)
+                if (s - 1) // 2 >= PD:
+                    sig_z(s - 1)
+                elif s % 2 == 0:
+                    sig_z(s - 2)
+                    sig_z(s - 1)
+            if main and s % 2 == 1 and p < PD:
+                tt("pool", un, un, u["qn"][:], ALU.add)
+                tt("pool", pp["uz"][:], pp["uz"][:], pp["vz"][:], ALU.add)
+            if s % 2 == 1 and 1 <= p <= PD:
+                mul_z("pool", p - 1, 0, 2)
+            if s % 2 == 0 and 1 <= p <= LASTP:
+                sub_h("pool", p - 1, 0, 2)
+                if p - 1 >= PD:
+                    mul_z("pool", p - 1, 0, 2)
+            if s == NSLOT - 1:
+                sub_h("pool", LASTP, 0, 1)
+                mul_z("pool", LASTP, 0, 1)
+            if s == NSLOT:
+                sub_h("dve", LASTP, 1, 2)
+                mul_z("dve", LASTP, 1, 2)
+
+        def tanh_of(s):
+            c1, bh1, e1 = unit_of(s)
+            un1 = pr[s // 2]["un"][:, e1, :]
+            nc.scalar.activation(out=un1, in_=un1, func=AF.Tanh, bias=b_in[:, c1, e1:e1 + 1], scale=1.0)
+
+        def sig_z(s):
+            c1, bh1, e1 = unit_of(s)
+            uz1 = pr[s // 2]["uz"][:, e1, :]
+            nc.scalar.activation(out=uz1, in_=uz1, func=AF.Sigmoid, bias=b_zn[:, c1, e1:e1 + 1], scale=-1.0)
+
+        pe_ra(0)()
+        for s in range(NSLOT + 2):
+            slot(s)
+            if s == 0:
+                for t in range(4, 8):
+                    run_job(job_h(t), "act" if t % 2 == 0 else "dve")
+                quant_h(0, 1)
+                quant_h(1, 1)

@@ -16,32 +16,23 @@ B = 1024
 H = 1024
 IN = 258
 NB = 512
-NSLOT = 16
-O_AT = {8: [(0, 0)], 9: [(0, 1)], 10: [(0, 2)], 11: [(0, 3), (0, 4)], 12: [(0, 5)], 13: [(0, 6), (0, 7)],
-        15: [(1, 0), (1, 1)], 16: [(1, 2), (1, 3)], 17: [(1, 4), (1, 5), (1, 6), (1, 7)]}
-PD = 2
-LASTP = NSLOT // 2 - 1
+NSTEP = 16
+ONE = 16
+WROW = 800
 FLOPS = 2 * B * 3 * H * (H + IN)
 
 
-def weave(ms, ts, late):
-    gaps = len(ms) - 1
-    total = len(ts) + len(late)
-    first = list(ts)
-    second = list(late)
+def weave(ms, ts):
     done = 0
     for i, m in enumerate(ms):
         m()
-        if i < gaps:
-            hi = ((i + 1) * total + gaps - 1) // gaps
-            while done < hi:
-                if i >= 3 and len(second) > 0:
-                    second.pop(0)()
-                elif len(first) > 0:
-                    first.pop(0)()
-                else:
-                    break
-                done += 1
+        hi = ((i + 1) * len(ts) + len(ms) - 1) // len(ms)
+        while done < hi:
+            ts[done]()
+            done += 1
+    while done < len(ts):
+        ts[done]()
+        done += 1
 
 
 def tile_wavernncell_pa_kernel(tc, x, feat, aux1, h, w_ih, w_hh, b_ih, b_hh, out):
@@ -51,27 +42,26 @@ def tile_wavernncell_pa_kernel(tc, x, feat, aux1, h, w_ih, w_hh, b_ih, b_hh, out
         const = ctx.enter_context(tc.tile_pool(name="const", bufs=1))
         wpool = ctx.enter_context(tc.tile_pool(name="wpool", bufs=2))
         work = ctx.enter_context(tc.tile_pool(name="work", bufs=2))
-        acc = ctx.enter_context(tc.psum_pool(name="acc", bufs=5))
-        tp = ctx.enter_context(tc.psum_pool(name="tp", bufs=3))
+        acc = ctx.enter_context(tc.psum_pool(name="acc", bufs=6))
+        tp = ctx.enter_context(tc.psum_pool(name="tp", bufs=2))
 
+        x_v = x.rearrange("(t p) c -> p t c", p=P)
         feat_v = feat.rearrange("(t p) k -> p t k", p=P)
         aux_v = aux1.rearrange("(t p) k -> p t k", p=P)
-        x_v = x.rearrange("(t p) c -> p t c", p=P)
         h_v = h.rearrange("(t p) k -> p t k", p=P)
         out_v = out.rearrange("(t p) j -> p t j", p=P)
-        wih_v = w_ih.rearrange("(G g q d e) k -> g d q G (e k)", G=3, g=2, q=P, d=2, e=2)
-        whh_v = w_hh.rearrange("(G g q d e) k -> g d q G (e k)", G=3, g=2, q=P, d=2, e=2)
-        bih_v = b_ih.rearrange("(m q f) -> q m f", m=6, q=P, f=4)
-        bhh_v = b_hh.rearrange("(m q f) -> q m f", m=6, q=P, f=4)
+        wih_v = w_ih.rearrange("(G c e p) k -> c e p G k", G=3, c=4, e=2, p=P)
+        whh_v = w_hh.rearrange("(G c e p) k -> c G p e k", G=3, c=4, e=2, p=P)
+        bih_v = b_ih.rearrange("(m u) -> m u", u=P)
+        bhh_v = b_hh.rearrange("(m u) -> m u", u=P)
 
         ident_f = const.tile([P, P], F32, name="ident_f")
         ident_b = const.tile([P, P], BF16, name="ident_b")
         warm = const.tile([P, 1], F32, name="warm")
-        fn = const.tile([P, 8, P], BF16, name="fn")
-        an = const.tile([P, 8, P], BF16, name="an")
+        fan = const.tile([P, 8, 2 * P], BF16, name="fan")
         xn = const.tile([P, 8, P], BF16, name="xn")
-        feat_t = const.tile([P, B], BF16, name="feat_t")
-        aux_t = const.tile([P, B], BF16, name="aux_t")
+        bn = const.tile([P, P], BF16, name="bn")
+        fa_t = const.tile([P, 2, B], BF16, name="fa_t")
         x_t = const.tile([P, B], BF16, name="x_t")
         xb = const.tile([P, 2 * B], BF16, name="xb")
         hn = const.tile([P, 8, H], BF16, name="hn")
@@ -79,58 +69,60 @@ def tile_wavernncell_pa_kernel(tc, x, feat, aux1, h, w_ih, w_hh, b_ih, b_hh, out
         hc = const.tile([P, 2, B], U32, name="hc", align_bytes=64)
         hs = const.tile([P, 2, B], U8, name="hs", align_bytes=64)
         wx = const.tile([P, 4, 3, P], BF16, name="wx")
-        bi = const.tile([P, 12, 2], BF16, name="bi")
-        bh2 = const.tile([P, 12, 2], BF16, name="bh2")
-        b_r = const.tile([P, 4, 2], F32, name="b_r")
-        b_zn = const.tile([P, 4, 2], F32, name="b_zn")
-        b_in = const.tile([P, 4, 2], F32, name="b_in")
-        b_hn = const.tile([P, 4, 2], F32, name="b_hn")
+        wx_t = const.tile([P, 4, 3, P], BF16, name="wx_t")
+        b_t = const.tile([P, 48], F32, name="b_t")
+        b_r = const.tile([P, 8], F32, name="b_r")
+        b_z = const.tile([P, 8], F32, name="b_z")
 
         wt = {}
         ut = {}
-        pr = {}
-        ft = {}
-        ra = {}
+        bt = {}
 
-        def load_w(c):
-            win = wpool.tile([P, 3, 2 * IN], BF16, name="win", tag="win")
-            wn = wpool.tile([P, 3, 2 * H], BF16, name="wn", tag="wn")
-            if c == 0:
-                nc.sync.dma_start(out=win[:], in_=wih_v[c // 2, c % 2])
-            for G in range(3):
-                nc.sync.dma_start(out=wn[:, G, :], in_=whh_v[c // 2, c % 2, :, G, :])
-            if c > 0:
-                nc.sync.dma_start(out=win[:], in_=wih_v[c // 2, c % 2])
+        def load_whh(c, G):
+            nc.sync.dma_start(out=wt[c]["wn"][:, G, :, :], in_=whh_v[c, G])
+
+        def load_wih(c):
+            for e in range(2):
+                nc.sync.dma_start(out=wt[c]["win"][:, e, 0:3 * IN].rearrange("p (G k) -> p G k", k=IN), in_=wih_v[c, e])
+
+        def new_w(c):
+            win = wpool.tile([P, 2, WROW], BF16, name="win", tag="win")
+            wn = wpool.tile([P, 3, 2, H], BF16, name="wn", tag="wn")
             wt[c] = {"win": win, "wn": wn}
 
         nc.vector.memset(warm[:], 0.0)
         nc.vector.memset(xn[:], 0.0)
+        nc.vector.memset(xn[:, :, ONE:ONE + 1], 1.0)
+        nc.vector.memset(bn[:], 0.0)
         nc.vector.memset(wx[:], 0.0)
-        make_identity(nc, ident_b[:])
         make_identity(nc, ident_f[:])
-        nc.sync.dma_start(out=fn[:], in_=feat_v)
-        nc.sync.dma_start(out=an[:], in_=aux_v)
-        with nc.allow_non_contiguous_dma(reason="small vectors, four bytes a piece"):
-            nc.scalar.dma_start(out=xn[:, :, 0:2], in_=x_v)
-            nc.scalar.dma_start(out=bi[:].rearrange("p (m d) e -> p m (d e)", d=2), in_=bih_v)
-            nc.scalar.dma_start(out=bh2[:].rearrange("p (m d) e -> p m (d e)", d=2), in_=bhh_v)
-        nc.scalar.dma_start(out=xb[:], in_=x.rearrange("b c -> (b c)").partition_broadcast(P))
-        nc.scalar.activation(out=warm[:], in_=warm[:], func=AF.Sigmoid)
-        win0 = wpool.tile([P, 3, 2 * IN], BF16, name="win", tag="win")
-        nc.sync.dma_start(out=win0[:], in_=wih_v[0, 0])
+        make_identity(nc, ident_b[:])
+        new_w(0)
+        new_w(1)
         for k in range(2):
             nc.sync.dma_start(out=hn[:, 2 * k:2 * k + 2, :], in_=h_v[:, 2 * k:2 * k + 2, :])
-        wn0 = wpool.tile([P, 3, 2 * H], BF16, name="wn", tag="wn")
-        for G in range(3):
-            nc.sync.dma_start(out=wn0[:, G, :], in_=whh_v[0, 0, :, G, :])
+        load_whh(0, 0)
+        nc.sync.dma_start(out=fan[:, :, 0:P], in_=feat_v)
+        nc.sync.dma_start(out=fan[:, :, P:2 * P], in_=aux_v)
+        load_wih(0)
+        with nc.allow_non_contiguous_dma(reason="x: four bytes a piece"):
+            nc.scalar.dma_start(out=xn[:, :, 0:2], in_=x_v)
+        nc.scalar.dma_start(out=bn[0:24, :], in_=bih_v)
+        nc.scalar.dma_start(out=bn[24:48, :], in_=bhh_v)
+        load_whh(0, 1)
+        load_whh(0, 2)
+        nc.sync.dma_start(out=xb[:], in_=x.rearrange("b c -> (b c)").partition_broadcast(P))
         for k in range(2, 4):
             nc.sync.dma_start(out=hn[:, 2 * k:2 * k + 2, :], in_=h_v[:, 2 * k:2 * k + 2, :])
-        wt[0] = {"win": win0, "wn": wn0}
-        load_w(1)
+        for G in range(3):
+            load_whh(1, G)
+        load_wih(1)
+        nc.scalar.activation(out=warm[:], in_=warm[:], func=AF.Sigmoid)
 
         xb_v = xb[:].rearrange("p (b c) -> p b c", c=2)
         hn_w = hn[:].bitcast(F32)
         hg_w = hg[:].bitcast(F32)
+        fan_w = fan[:].bitcast(F32)
 
         def copy_on(eng, dst, src):
             if eng == "act":
@@ -141,54 +133,64 @@ def tile_wavernncell_pa_kernel(tc, x, feat, aux1, h, w_ih, w_hh, b_ih, b_hh, out
         def tr(dst, src, ident):
             return lambda: nc.tensor.transpose(dst, src, ident[:])
 
-        def job_rows(src, dst):
-            pt = tp.tile([P, 8, P], BF16, name="pt_f", tag="tp")
-            ts = [tr(pt[:, t, :], src[:, t, :], ident_b) for t in range(8)]
-            return ts, lambda eng: copy_on(eng, dst[:], pt[:].rearrange("p t b -> p (t b)"))
+        def job_fa(pool, tag, i):
+            pt = pool.tile([P, 4, P], F32, name="pt_f", tag=tag)
+            ts = [tr(pt[:, t, :], fan_w[:, 4 * i + t, :], ident_f) for t in range(4)]
+            src = pt[:].rearrange("p t b -> p (t b)").bitcast(BF16).rearrange("p (b r) -> p r b", r=2)
+            return ts, lambda eng: copy_on(eng, fa_t[:, :, NB * i:NB * (i + 1)], src)
 
-        def job_h(t):
-            pt = tp.tile([P, 4, P], F32, name="pt_h", tag="tp")
-            ts = [tr(pt[:, wb, :], hn_w[:, t, 256 * (wb // 2) + wb % 2:256 * (wb // 2 + 1):2], ident_f) for wb in range(4)]
+        def job_x(pool, tag):
+            pt = pool.tile([P, 8, P], BF16, name="pt_x", tag=tag)
+            ts = [tr(pt[:, t, :], xn[:, t, :], ident_b) for t in range(8)]
+            return ts, lambda eng: copy_on(eng, x_t[:], pt[:].rearrange("p t b -> p (t b)"))
+
+        def job_bias(pool, tag):
+            pt = pool.tile([P, P], BF16, name="pt_b", tag=tag)
+            return [tr(pt[:], bn[:], ident_b)], lambda eng: copy_on(eng, b_t[:], pt[:, 0:48])
+
+        def job_h(pool, tag, t):
+            pt = pool.tile([P, 4, P], F32, name="pt_h", tag=tag)
+            ts = [tr(pt[:, 2 * g + u, :], hn_w[:, t, 256 * g + u:256 * (g + 1):2], ident_f)
+                  for g in range(2) for u in range(2)]
             return ts, lambda eng: copy_on(eng, hg_w[:, :, t * P:(t + 1) * P, :],
                                            pt[:].rearrange("p (g u) b -> p g b u", g=2))
 
         def begin_w(c):
             w = wt[c]
-            w["w01"] = wpool.tile([P, 3, 2, 2], F32, name="w01", tag="w01")
-            w["wit"] = wpool.tile([P, 15, P], BF16, name="wit", tag="wit")
+            w["w01"] = wpool.tile([P, 3, 2, 2], F32, name="w01", tag="w01", bufs=3)
+            w["wit"] = wpool.tile([P, 2, 6, P], BF16, name="wit", tag="wit", bufs=3)
             w["wg"] = wpool.tile([P, 6, 2, P, 4], BF16, name="wg", tag="wg", align_bytes=64)
             w["wc"] = wpool.tile([P, 6, 2, P], U32, name="wc", tag="wc", align_bytes=64)
             w["ws"] = wpool.tile([P, 6, 2, P], U8, name="ws", tag="ws", align_bytes=64)
 
         def small_w(c):
-            win_v = wt[c]["win"][:].rearrange("p G (e k) -> p G e k", e=2)
-            nc.scalar.copy(out=wt[c]["w01"][:], in_=win_v[:, :, :, 256:258])
-            nc.scalar.copy(out=wx[:, c, 0:2, 0:2], in_=win_v[:, 0, :, 256:258])
-            nc.scalar.copy(out=wx[:, c, 2, 0:2], in_=win_v[:, 2, 0, 256:258])
+            win = wt[c]["win"][:, :, 0:3 * IN].rearrange("p e (G k) -> p G e k", k=IN)
+            nc.scalar.copy(out=wt[c]["w01"][:], in_=win[:, :, :, 256:258])
+            nc.scalar.copy(out=wx[:, c, 0:2, 0:2], in_=win[:, 2, :, 256:258])
+            nc.scalar.copy(out=wx[:, c, 2, 0:2], in_=win[:, 1, 0, 256:258])
 
-        def job_ia(c):
-            win_v = wt[c]["win"][:].rearrange("p G (e k) -> p G e k", e=2)
+        def job_i(pool, tag, c, lo, hi):
+            win_w = wt[c]["win"][:].rearrange("p e k -> p (e k)").bitcast(F32)
             wit = wt[c]["wit"]
-            pt = tp.tile([P, 8, P], BF16, name="pt_a", tag="tp")
-            ts = [tr(pt[:, i, :], win_v[:, i // 4, (i // 2) % 2, (i % 2) * P:(i % 2 + 1) * P], ident_b)
-                  for i in range(8)]
-            return ts, lambda eng: copy_on(eng, wit[:, 0:8, :], pt[:])
+            pt = pool.tile([P, 4, P], F32, name="pt_i", tag=tag)
+            ts = [tr(pt[:, i - lo, :], win_w[:, WROW // 2 * (i % 2) + 129 * (i // 2):WROW // 2 * (i % 2) + 129 * (i // 2) + P], ident_f)
+                  for i in range(lo, hi)]
+            src = pt[:, 0:hi - lo, :].rearrange("p i u -> p (i u)").bitcast(BF16).rearrange(
+                "p (i u r) -> p r i u", u=P, r=2)
+            return ts, lambda eng: copy_on(eng, wit[:, :, lo:hi, :], src)
 
-        def job_ib(c):
-            win_v = wt[c]["win"][:].rearrange("p G (e k) -> p G e k", e=2)
-            wit = wt[c]["wit"]
-            pt = tp.tile([P, 8, P], BF16, name="pt_b", tag="tp")
-            ts = [tr(pt[:, i, :], win_v[:, 2, i // 2, (i % 2) * P:(i % 2 + 1) * P], ident_b) for i in range(4)]
-            ts.extend([tr(pt[:, 4 + i, :], wx[:, c, i, :], ident_b) for i in range(3)])
-            return ts, lambda eng: copy_on(eng, wit[:, 8:15, :], pt[:, 0:7, :])
+        def job_wx(pool, tag, c):
+            pt = pool.tile([P, 3, P], BF16, name="pt_wx", tag=tag)
+            ts = [tr(pt[:, i, :], wx[:, c, i, :], ident_b) for i in range(3)]
+            return ts, lambda eng: copy_on(eng, wx_t[:, c, :, :], pt[:])
 
-        def job_w(c, ge):
+        def job_w(pool, tag, c, ge):
             wn_w = wt[c]["wn"][:].bitcast(F32)
             wg_w = wt[c]["wg"][:].bitcast(F32)
             G, e = ge // 2, ge % 2
-            pt = tp.tile([P, 4, P], F32, name="pt_w", tag="tp")
-            ts = [tr(pt[:, wb, :], wn_w[:, G, e * 512 + 256 * (wb // 2) + wb % 2:e * 512 + 256 * (wb // 2 + 1):2], ident_f)
-                  for wb in range(4)]
+            pt = pool.tile([P, 4, P], F32, name="pt_w", tag=tag)
+            ts = [tr(pt[:, 2 * g + u, :], wn_w[:, G, e, 256 * g + u:256 * (g + 1):2], ident_f)
+                  for g in range(2) for u in range(2)]
             return ts, lambda eng: copy_on(eng, wg_w[:, ge, :, :, :],
                                            pt[:].rearrange("p (g u) q -> p g q u", g=2))
 
@@ -204,112 +206,6 @@ def tile_wavernncell_pa_kernel(tc, x, feat, aux1, h, w_ih, w_hh, b_ih, b_hh, out
             nc.vector.quantize_mx(out=hc[:, g, bs].bitcast(FP8X4), scales=hs[:, g, bs],
                                   in_=hg[:, g, bs, :].rearrange("p b t -> p (b t)"))
 
-        def job_o(g, t):
-            js = slice(512 * g, 512 * (g + 1))
-            pt = tp.tile([P, 4, P], F32, name="pt_o", tag="tp")
-            ts = [tr(pt[:, 2 * d + e, :], ft[2 * g + d][:, e, t * P:(t + 1) * P], ident_f)
-                  for d in range(2) for e in range(2)]
-
-            def ev(eng):
-                o_t = work.tile([P, 512], F32, name="o_t", tag="o_t", bufs=4)
-                nc.vector.tensor_tensor(out=o_t[:].rearrange("p (q f) -> p q f", f=4),
-                                        in0=pt[:].rearrange("p f q -> p q f"),
-                                        in1=hn[:, t, js].rearrange("p (q f) -> p q f", f=4),
-                                        op=ALU.add)
-                nc.sync.dma_start(out=out_v[:, t, js], in_=o_t[:])
-            return ts, ev
-
-        def run_job(job, eng):
-            for t in job[0]:
-                t()
-            job[1](eng)
-
-        begin_w(0)
-        run_job(job_rows(fn, feat_t), "act")
-        run_job(job_rows(an, aux_t), "dve")
-        small_w(0)
-        run_job(job_ia(0), "act")
-        run_job(job_ib(0), "dve")
-        run_job(job_rows(xn, x_t), "act")
-        for t in range(4):
-            run_job(job_h(t), "act" if t % 2 == 0 else "dve")
-        for ge in range(6):
-            run_job(job_w(0, ge), "act" if ge % 2 == 0 else "dve")
-            if ge == 0:
-                quant_h(0, 0)
-                quant_h(1, 0)
-            if ge == 3:
-                quant_w(0, 0)
-            if ge == 5:
-                quant_w(0, 1)
-        quant_w(0, 2)
-        nc.vector.tensor_tensor(out=b_r[:], in0=bi[:, 0:4, :], in1=bh2[:, 0:4, :], op=ALU.add)
-        nc.vector.scalar_tensor_tensor(out=b_zn[:], in0=bi[:, 4:8, :], scalar=-1.0, in1=bh2[:, 4:8, :],
-                                       op0=ALU.mult, op1=ALU.subtract)
-        nc.vector.tensor_copy(out=b_in[:], in_=bi[:, 8:12, :])
-        nc.vector.tensor_copy(out=b_hn[:], in_=bh2[:, 8:12, :])
-
-
-        def unit_of(s):
-            return s // 4, (s // 2) % 2, s % 2
-
-        def mm(ps, lhsT, rhs, start, stop):
-            return lambda: nc.tensor.matmul(ps[:], lhsT=lhsT, rhs=rhs, start=start, stop=stop)
-
-        def tacc(dst, src, stop):
-            return lambda: nc.tensor.matmul(dst, lhsT=src, rhs=ident_f[:], is_transpose=True, start=False, stop=stop)
-
-        def pe_ra(s):
-            c, bh, e = unit_of(s)
-            wc, ws = wt[c]["wc"], wt[c]["ws"]
-            ps = acc.tile([P, 4, P], F32, name="gra", tag="acc")
-            for i in range(4):
-                cs = slice(bh * NB + i * P, bh * NB + (i + 1) * P)
-                for kg in range(2):
-                    nc.tensor.matmul_mx(ps[:, i, :], lhsT=hc[:, kg, cs].bitcast(FP8X4), lhsT_scale=hs[:, kg, cs],
-                                        rhs=wc[:, e, kg, :].bitcast(FP8X4), rhs_scale=ws[:, e, kg, :],
-                                        start=(kg == 0), stop=(kg == 1))
-            ra[s] = work.tile([P, 4, P], F32, name="grs", tag="grs", bufs=2)
-            return lambda: nc.scalar.copy(out=ra[s][:], in_=ps[:])
-
-        def pe_unit(s, ts):
-            c, bh, e = unit_of(s)
-            w = wt[c]
-            wit, wc, ws = w["wit"], w["wc"], w["ws"]
-            bs = slice(bh * NB, (bh + 1) * NB)
-            gi_r = acc.tile([P, NB], F32, name="gi_r", tag="acc")
-            gi_z = acc.tile([P, NB], F32, name="gi_z", tag="acc")
-            gi_n = acc.tile([P, NB], F32, name="gi_n", tag="acc")
-            ms = [mm(gi_r, wit[:, 2 * e, :], feat_t[:, bs], True, False),
-                  mm(gi_r, wit[:, 2 * e + 1, :], aux_t[:, bs], False, False),
-                  mm(gi_r, wit[:, 12 + e, :], x_t[:, bs], False, False),
-                  mm(gi_z, wit[:, 4 + 2 * e, :], feat_t[:, bs], True, False),
-                  mm(gi_z, wit[:, 4 + 2 * e + 1, :], aux_t[:, bs], False, True),
-                  mm(gi_n, wit[:, 8 + 2 * e, :], feat_t[:, bs], True, False),
-                  mm(gi_n, wit[:, 8 + 2 * e + 1, :], aux_t[:, bs], False, e == 1)]
-            if e == 0:
-                ms.append(mm(gi_n, wit[:, 14, :], x_t[:, bs], False, True))
-            grs = ra[s]
-            late = [tacc(gi_r[:, i * P:(i + 1) * P], grs[:, i, :], i == 3) for i in range(4)]
-            weave(ms, ts, late)
-            gh = {}
-            for G in (2, 1):
-                ps = acc.tile([P, NB], F32, name="gh%d" % G, tag="acc")
-                for kg in range(2):
-                    nc.tensor.matmul_mx(ps[:], lhsT=wc[:, 2 * G + e, kg, :].bitcast(FP8X4),
-                                        lhsT_scale=ws[:, 2 * G + e, kg, :],
-                                        rhs=hc[:, kg, bs].bitcast(FP8X4), rhs_scale=hs[:, kg, bs],
-                                        start=(kg == 0), stop=(kg == 1))
-                gh[G] = ps
-            ra_out = pe_ra(s + 1) if s + 1 < NSLOT else None
-            if e == 0:
-                pr[s // 2] = {"un": work.tile([P, 2, NB], F32, name="un", tag="un", bufs=4),
-                              "uz": work.tile([P, 2, NB], F32, name="uz", tag="uz", bufs=4),
-                              "vz": work.tile([P, 2, NB], F32, name="vz", tag="vz", bufs=2)}
-            ut[s] = {"ra_out": ra_out, "gi_r": gi_r, "gi_n": gi_n, "gi_z": gi_z, "gh": gh,
-                     "ar": work.tile([P, NB], F32, name="ar", tag="ar", bufs=2),
-                     "qn": work.tile([P, NB], F32, name="qn", tag="qn", bufs=3)}
-
         def stt(dst, in0, scalar, in1, op0, op1):
             nc.vector.scalar_tensor_tensor(out=dst, in0=in0, scalar=scalar, in1=in1, op0=op0, op1=op1)
 
@@ -319,133 +215,237 @@ def tile_wavernncell_pa_kernel(tc, x, feat, aux1, h, w_ih, w_hh, b_ih, b_hh, out
             else:
                 nc.gpsimd.tensor_tensor(out=dst, in0=in0, in1=in1, op=op)
 
-        def h_t(p, i):
-            c, bh = p // 2, p % 2
-            return hg[:, c // 2, bh * NB:(bh + 1) * NB, 2 * (c % 2) + i]
+        def unit_of(s):
+            return s // 4, (s // 2) % 2, s % 2
 
-        def sub_h(eng, p, lo, hi):
-            un = pr[p]["un"]
-            for i in range(lo, hi):
-                tt(eng, un[:, i, :], un[:, i, :], h_t(p, i), ALU.subtract)
+        def mm(ps, lhsT, rhs, start, stop):
+            return lambda: nc.tensor.matmul(ps, lhsT=lhsT, rhs=rhs, start=start, stop=stop)
 
-        def mul_z(eng, p, lo, hi):
-            c, bh = p // 2, p % 2
-            if c not in ft:
-                ft[c] = work.tile([P, 2, B], F32, name="f_t", tag="f_t", bufs=4)
-            for i in range(lo, hi):
-                tt(eng, ft[c][:, i, bh * NB:(bh + 1) * NB], pr[p]["uz"][:, i, :], pr[p]["un"][:, i, :], ALU.mult)
+        def tacc(dst, src, stop):
+            return lambda: nc.tensor.matmul(dst, lhsT=src, rhs=ident_f[:], is_transpose=True, start=False, stop=stop)
 
-        def prep_jobs(s):
-            c, k = s // 4 + 1, s % 4
-            if c > 3:
-                return []
-            seq = [("w", c, ge) for ge in range(6)] + [("ia", c, 0), ("ib", c, 0)]
-            cuts = (0, 0, 3, 6, 8) if c == 1 else (0, 2, 4, 6, 8)
-            return seq[cuts[k]:cuts[k + 1]]
+        def begin_unit(s):
+            ut[s] = {"gi_r": acc.tile([P, NB], F32, name="gi_r", tag="acc")}
 
-        def make_job(d):
-            if d[0] == "w":
-                if d[2] == 0:
-                    begin_w(d[1])
-                return job_w(d[1], d[2])
-            if d[0] == "ia":
-                return job_ia(d[1])
-            if d[0] == "ib":
-                return job_ib(d[1])
-            return job_o(d[1], d[2])
-
-        def slot(s):
+        def pe_gi_r(s):
             c, bh, e = unit_of(s)
-            k = s % 4
-            p = s // 2
-            main = s < NSLOT
-            if main and k == 0 and c + 2 < 4:
-                load_w(c + 2)
-            jobs = [make_job(d) for d in prep_jobs(s)] if main else []
-            ojobs = [job_o(co, io) for co, io in O_AT.get(s, [])]
+            wit = wt[c]["wit"]
+            bs = slice(bh * NB, (bh + 1) * NB)
+            ps = ut[s]["gi_r"]
+            return [mm(ps[:], wit[:, r, e, :], fa_t[:, r, bs], r == 0, r == 1) for r in range(2)]
+
+        def pe_mx(s):
+            c, bh, e = unit_of(s)
+            wc, ws = wt[c]["wc"], wt[c]["ws"]
+            bs = slice(bh * NB, (bh + 1) * NB)
+            for G in (0, 1, 2):
+                ps = acc.tile([P, NB], F32, name="gh%d" % G, tag="acc")
+                for kg in range(2):
+                    nc.tensor.matmul_mx(ps[:], lhsT=wc[:, 2 * G + e, kg, :].bitcast(FP8X4),
+                                        lhsT_scale=ws[:, 2 * G + e, kg, :],
+                                        rhs=hc[:, kg, bs].bitcast(FP8X4), rhs_scale=hs[:, kg, bs],
+                                        start=(kg == 0), stop=(kg == 1))
+                ut[s]["gh%d" % G] = ps
+
+        def pe_b(b):
+            m, j = b // 2, b % 2
+            c, bh = m // 2, m % 2
+            wit = wt[c]["wit"]
+            gz = acc.tile([P, 2, 256], F32, name="gz", tag="acc")
+            gn = acc.tile([P, 2, 256], F32, name="gn", tag="acc")
+            bt[b] = {"gz": gz, "gn": gn}
+            seq = []
+            for k in range(2):
+                t = 4 * bh + 2 * j + k
+                cols = slice(t * P, (t + 1) * P)
+                loc = slice((2 * j + k) * P, (2 * j + k + 1) * P)
+                wz = [wit[:, r, 2:4, :].rearrange("p e u -> p (e u)") for r in range(2)]
+                wn = [wit[:, r, 4:6, :].rearrange("p e u -> p (e u)") for r in range(2)]
+                wnx = wx_t[:, c, 0:2, :].rearrange("p e u -> p (e u)")
+                tz = [tacc(gz[:, k, e * P:(e + 1) * P], ut[2 * m + e]["zc"][:, loc], e == 1) for e in range(2)]
+                tn = [tacc(gn[:, k, e * P:(e + 1) * P], ut[2 * m + e]["rq"][:, loc], e == 1) for e in range(2)]
+                z = [mm(gz[:, k, :], fa_t[:, r, cols], wz[r], r == 0, False) for r in range(2)]
+                z.append(mm(gz[:, k, 0:P], x_t[:, cols], wx_t[:, c, 2, :], False, False))
+                n = [mm(gn[:, k, :], fa_t[:, r, cols], wn[r], r == 0, False) for r in range(2)]
+                n.append(mm(gn[:, k, :], x_t[:, cols], wnx, False, False))
+                seq.append((z, n, tz, tn))
+            return seq
+
+        def plain(k, prep_ts):
+            r = []
+            if k + 1 < NSTEP:
+                begin_unit(k + 1)
+                r = pe_gi_r(k + 1)
+            if k < 2:
+                weave(r, prep_ts)
+                return
+            (z, n, tz, tn), (z2, n2, tz2, tn2) = pe_b(k - 2)
+            ms = [z[0], n[0], z[1], n[1], z[2], n[2]]
+            for i in range(2):
+                if r:
+                    ms.append(r[i])
+                ms.append(tz[i])
+            ms.extend([z2[0], tn[0], z2[1], tn[1], n2[0], z2[2], n2[1], tz2[0], n2[2], tz2[1], tn2[0], tn2[1]])
+            weave(ms, prep_ts)
+
+        def acts_b(b):
+            z = work.tile([P, 2, 256], F32, name="zt", tag="zt", bufs=3)
+            n = work.tile([P, 2, 256], F32, name="nt", tag="nt", bufs=4)
+            nc.scalar.activation(out=z[:], in_=bt[b]["gz"][:], func=AF.Sigmoid, scale=-1.0)
+            nc.scalar.activation(out=n[:], in_=bt[b]["gn"][:], func=AF.Tanh)
+            bt[b]["z"] = z
+            bt[b]["n"] = n
+
+        def h_of(b):
+            m, j = b // 2, b % 2
+            c, bh = m // 2, m % 2
+            t = 4 * bh + 2 * j
+            return hn[:, t:t + 2, 256 * c:256 * (c + 1)], out_v[:, t:t + 2, 256 * c:256 * (c + 1)]
+
+        def sub_mul_b(b, eng):
+            hv = h_of(b)[0]
+            n, z = bt[b]["n"], bt[b]["z"]
+            tt(eng, n[:], n[:], hv, ALU.subtract)
+            tt(eng, n[:], z[:], n[:], ALU.mult)
+
+        def out_b(b):
+            hv, ov = h_of(b)
+            o = work.tile([P, 2, 256], F32, name="ot", tag="ot", bufs=3)
+            tt("dve", o[:], bt[b]["n"][:], hv, ALU.add)
+            nc.sync.dma_start(out=ov, in_=o[:])
+
+        def prep_jobs(k):
+            c = k // 4 + 1
+            if k >= NSTEP or c > 3:
+                return []
+            w = [("w", c, ge) for ge in range(6)]
+            if c == 1:
+                return [[("h", t, 0) for t in range(4, 8)], w[0:4], w[4:6] + [("ia", c, 0)],
+                        [("ib", c, 0), ("wx", c, 0)]][k % 4]
+            return [w[0:2], w[2:4] + [("ia", c, 0)], w[4:6], [("ib", c, 0), ("wx", c, 0)]][k % 4]
+
+        def make_job(d, pool, tag):
+            kind, c, i = d
+            if kind == "w":
+                if i == 0:
+                    begin_w(c)
+                return job_w(pool, tag, c, i)
+            if kind == "h":
+                return job_h(pool, tag, c)
+            if kind == "ia":
+                return job_i(pool, tag, c, 0, 4)
+            if kind == "ib":
+                return job_i(pool, tag, c, 4, 6)
+            return job_wx(pool, tag, c)
+
+        def quants(k):
+            for kind, c, i in prep_jobs(k - 1) if k > 0 else []:
+                if kind == "w" and i % 2 == 1:
+                    quant_w(c, i // 2)
+                if kind == "h" and c == 7:
+                    quant_h(0, 1)
+                    quant_h(1, 1)
+
+        def step(k):
+            main = k < NSTEP
+            if main:
+                pe_mx(k)
+            if main and k % 4 == 2 and k // 4 + 1 < 4:
+                small_w(k // 4 + 1)
+            jobs = [make_job(d, tp, "tp") for d in prep_jobs(k)[0:2]]
+            late = prep_jobs(k)[2:]
             ts = []
-            for j in jobs + ojobs:
+            for j in jobs:
                 ts.extend(j[0])
             if main:
-                pe_unit(s, ts)
-                u = ut[s]
-                pp = pr[p]
+                u = ut[k]
+                c, bh, e = unit_of(k)
+                i = 2 * c + e
                 w01 = wt[c]["w01"]
                 bs = slice(bh * NB, (bh + 1) * NB)
-                x0 = xb_v[:, bs, 0]
-                x1 = xb_v[:, bs, 1]
-                un = pp["un"][:, e, :]
-                uz = pp["uz"][:, e, :]
-                vz = pp["vz"][:, e, :]
-                ar = u["ar"]
-                nc.scalar.activation(out=ar[:], in_=u["gi_r"][:], func=AF.Sigmoid, bias=b_r[:, c, e:e + 1], scale=1.0)
-                for j in jobs:
-                    j[1]("act")
-                if u["ra_out"] is not None:
-                    u["ra_out"]()
-                if c + 1 < 4 and k == 2:
-                    small_w(c + 1)
-                for d in prep_jobs(s - 1) if s > 0 else []:
-                    if d[0] == "w" and d[2] % 2 == 1:
-                        quant_w(d[1], d[2] // 2)
-                stt(uz, x0, w01[:, 1, e, 0:1], u["gi_z"][:], ALU.mult, ALU.add)
-                if e == 1:
-                    stt(un, x0, w01[:, 2, e, 0:1], u["gi_n"][:], ALU.mult, ALU.add)
-                if e == 1:
-                    stt(un, x1, w01[:, 2, e, 1:2], un, ALU.mult, ALU.add)
-                stt(u["qn"][:], u["gh"][2][:], b_hn[:, c, e:e + 1], ar[:], ALU.add, ALU.mult)
+                x0, x1 = xb_v[:, bs, 0], xb_v[:, bs, 1]
+                zc = work.tile([P, NB], F32, name="zc", tag="zc", bufs=5)
+                u["zc"] = zc
                 if e == 0:
-                    tt("dve", un, u["gi_n"][:], u["qn"][:], ALU.add)
-                stt(vz, x1, w01[:, 1, e, 1:2], u["gh"][1][:], ALU.mult, ALU.add)
-                for j in ojobs:
-                    j[1]("dve")
-                if p >= PD:
-                    if e == 1:
-                        tt("dve", un, un, u["qn"][:], ALU.add)
-                    tt("dve", uz, uz, vz, ALU.add)
-            else:
-                for t in ts:
+                    nc.scalar.activation(out=zc[:], in_=u["gh1"][:], func=AF.Identity, bias=b_z[:, i:i + 1], scale=1.0)
+                else:
+                    a1 = work.tile([P, NB], F32, name="a1", tag="a1", bufs=2)
+                    nc.scalar.activation(out=a1[:], in_=x1, func=AF.Identity, bias=b_z[:, i:i + 1],
+                                         scale=w01[:, 1, 1, 1:2])
+                ra = work.tile([P, NB], F32, name="ra", tag="ra", bufs=2)
+                rb = work.tile([P, NB], F32, name="rb", tag="rb", bufs=2)
+                rq = work.tile([P, NB], F32, name="rq", tag="rq", bufs=5)
+                u["rq"] = rq
+                stt(ra[:], x0, w01[:, 0, e, 0:1], u["gi_r"][:], ALU.mult, ALU.add)
+                if k >= 4:
+                    out_b(k - 4)
+                stt(rb[:], x1, w01[:, 0, e, 1:2], u["gh0"][:], ALU.mult, ALU.add)
+                if e == 1:
+                    stt(zc[:], x0, w01[:, 1, 1, 0:1], u["gh1"][:], ALU.mult, ALU.add)
+                tt("dve", ra[:], ra[:], rb[:], ALU.add)
+                quants(k)
+                nc.scalar.activation(out=ra[:], in_=ra[:], func=AF.Sigmoid, bias=b_r[:, i:i + 1], scale=1.0)
+                stt(rq[:], u["gh2"][:], b_t[:, 40 + i:41 + i], ra[:], ALU.add, ALU.mult)
+                if e == 1:
+                    tt("dve", zc[:], zc[:], a1[:], ALU.add)
+            elif k - 4 < NSTEP:
+                out_b(k - 4)
+            if k < NSTEP + 2:
+                plain(k, ts)
+            for j in jobs:
+                j[1]("act")
+            for d in late:
+                j = make_job(d, tp, "tp")
+                for t in j[0]:
                     t()
-                for j in ojobs:
-                    j[1]("dve")
-            if 1 <= s <= NSLOT:
-                tanh_of(s - 1)
-                if (s - 1) // 2 >= PD:
-                    sig_z(s - 1)
-                elif s % 2 == 0:
-                    sig_z(s - 2)
-                    sig_z(s - 1)
-            if main and s % 2 == 1 and p < PD:
-                tt("pool", un, un, u["qn"][:], ALU.add)
-                tt("pool", pp["uz"][:], pp["uz"][:], pp["vz"][:], ALU.add)
-            if s % 2 == 1 and 1 <= p <= PD:
-                mul_z("pool", p - 1, 0, 2)
-            if s % 2 == 0 and 1 <= p <= LASTP:
-                sub_h("pool", p - 1, 0, 2)
-                if p - 1 >= PD:
-                    mul_z("pool", p - 1, 0, 2)
-            if s == NSLOT - 1:
-                sub_h("pool", LASTP, 0, 1)
-                mul_z("pool", LASTP, 0, 1)
-            if s == NSLOT:
-                sub_h("dve", LASTP, 1, 2)
-                mul_z("dve", LASTP, 1, 2)
+                j[1]("act")
+            if 2 <= k < NSTEP + 2:
+                acts_b(k - 2)
+                sub_mul_b(k - 2, "pool" if k < NSTEP + 1 else "dve")
 
-        def tanh_of(s):
-            c1, bh1, e1 = unit_of(s)
-            un1 = pr[s // 2]["un"][:, e1, :]
-            nc.scalar.activation(out=un1, in_=un1, func=AF.Tanh, bias=b_in[:, c1, e1:e1 + 1], scale=1.0)
+        count = [0]
 
-        def sig_z(s):
-            c1, bh1, e1 = unit_of(s)
-            uz1 = pr[s // 2]["uz"][:, e1, :]
-            nc.scalar.activation(out=uz1, in_=uz1, func=AF.Sigmoid, bias=b_zn[:, c1, e1:e1 + 1], scale=-1.0)
+        def run_job(make, *args):
+            i = count[0]
+            count[0] = i + 1
+            job = make(tp, "tp", *args) if i % 4 == 3 else make(acc, "acc", *args)
+            for t in job[0]:
+                t()
+            job[1]("act" if i % 2 == 0 else "dve")
 
-        pe_ra(0)()
-        for s in range(NSLOT + 2):
-            slot(s)
-            if s == 0:
-                for t in range(4, 8):
-                    run_job(job_h(t), "act" if t % 2 == 0 else "dve")
-                quant_h(0, 1)
-                quant_h(1, 1)
+        begin_w(0)
+        for t in range(4):
+            run_job(job_h, t)
+        run_job(job_w, 0, 0)
+        run_job(job_w, 0, 1)
+        quant_h(0, 0)
+        quant_h(1, 0)
+        run_job(job_fa, 0)
+        run_job(job_fa, 1)
+        quant_w(0, 0)
+        small_w(0)
+        run_job(job_i, 0, 0, 4)
+        run_job(job_bias)
+        nc.vector.tensor_tensor(out=b_r[:], in0=b_t[:, 0:8], in1=b_t[:, 24:32], op=ALU.add)
+        nc.vector.tensor_tensor(out=b_z[:], in0=b_t[:, 8:16], in1=b_t[:, 32:40], op=ALU.add)
+        nc.vector.tensor_copy(out=wx[:, :, 0:2, ONE], in_=b_t[:, 16:24].rearrange("p (c e) -> p c e", e=2))
+        begin_unit(0)
+        for m in pe_gi_r(0):
+            m()
+        run_job(job_w, 0, 2)
+        run_job(job_w, 0, 3)
+        run_job(job_x)
+        quant_w(0, 1)
+        run_job(job_w, 0, 4)
+        run_job(job_w, 0, 5)
+        run_job(job_i, 0, 4, 6)
+        quant_w(0, 2)
+        run_job(job_wx, 0)
+
+        for k in range(NSTEP + 4):
+            if k % 4 == 0 and k < NSTEP and k // 4 + 2 < 4:
+                new_w(k // 4 + 2)
+                for G in range(3):
+                    load_whh(k // 4 + 2, G)
+                load_wih(k // 4 + 2)
+            step(k)

@@ -17,19 +17,24 @@ H = 1024
 IN = 258
 NB = 512
 NSTEP = 16
+NHEAD = 4
 ONE = 16
 WROW = 800
 FLOPS = 2 * B * 3 * H * (H + IN)
 
 
-def weave(ms, ts):
+def weave(ops, ts):
+    gaps = sum(1 for op in ops[:-1] if op[1])
+    seen = 0
     done = 0
-    for i, m in enumerate(ms):
-        m()
-        hi = ((i + 1) * len(ts) + len(ms) - 1) // len(ms)
-        while done < hi:
-            ts[done]()
-            done += 1
+    for i, op in enumerate(ops):
+        op[0]()
+        if op[1] and i < len(ops) - 1:
+            seen += 1
+            hi = (seen * len(ts) + gaps - 1) // gaps
+            while done < hi:
+                ts[done]()
+                done += 1
     while done < len(ts):
         ts[done]()
         done += 1
@@ -99,19 +104,19 @@ def tile_wavernncell_pa_kernel(tc, x, feat, aux1, h, w_ih, w_hh, b_ih, b_hh, out
         make_identity(nc, ident_b[:])
         new_w(0)
         new_w(1)
-        for k in range(2):
-            nc.sync.dma_start(out=hn[:, 2 * k:2 * k + 2, :], in_=h_v[:, 2 * k:2 * k + 2, :])
-        load_whh(0, 0)
         nc.sync.dma_start(out=fan[:, :, 0:P], in_=feat_v)
         nc.sync.dma_start(out=fan[:, :, P:2 * P], in_=aux_v)
         load_wih(0)
+        for k in range(2):
+            nc.sync.dma_start(out=hn[:, 2 * k:2 * k + 2, :], in_=h_v[:, 2 * k:2 * k + 2, :])
+        load_whh(0, 0)
+        nc.sync.dma_start(out=xb[:], in_=x.rearrange("b c -> (b c)").partition_broadcast(P))
         with nc.allow_non_contiguous_dma(reason="x: four bytes a piece"):
             nc.scalar.dma_start(out=xn[:, :, 0:2], in_=x_v)
         nc.scalar.dma_start(out=bn[0:24, :], in_=bih_v)
         nc.scalar.dma_start(out=bn[24:48, :], in_=bhh_v)
         load_whh(0, 1)
         load_whh(0, 2)
-        nc.sync.dma_start(out=xb[:], in_=x.rearrange("b c -> (b c)").partition_broadcast(P))
         for k in range(2, 4):
             nc.sync.dma_start(out=hn[:, 2 * k:2 * k + 2, :], in_=h_v[:, 2 * k:2 * k + 2, :])
         for G in range(3):
@@ -169,20 +174,30 @@ def tile_wavernncell_pa_kernel(tc, x, feat, aux1, h, w_ih, w_hh, b_ih, b_hh, out
             nc.scalar.copy(out=wx[:, c, 0:2, 0:2], in_=win[:, 2, :, 256:258])
             nc.scalar.copy(out=wx[:, c, 2, 0:2], in_=win[:, 1, 0, 256:258])
 
-        def job_i(pool, tag, c, lo, hi):
-            win_w = wt[c]["win"][:].rearrange("p e k -> p (e k)").bitcast(F32)
-            wit = wt[c]["wit"]
-            pt = pool.tile([P, 4, P], F32, name="pt_i", tag=tag)
-            ts = [tr(pt[:, i - lo, :], win_w[:, WROW // 2 * (i % 2) + 129 * (i // 2):WROW // 2 * (i % 2) + 129 * (i // 2) + P], ident_f)
-                  for i in range(lo, hi)]
-            src = pt[:, 0:hi - lo, :].rearrange("p i u -> p (i u)").bitcast(BF16).rearrange(
-                "p (i u r) -> p r i u", u=P, r=2)
-            return ts, lambda eng: copy_on(eng, wit[:, :, lo:hi, :], src)
+        def wih_words(c, i):
+            at = WROW // 2 * (i % 2) + 129 * (i // 2)
+            return wt[c]["win"][:].rearrange("p e k -> p (e k)").bitcast(F32)[:, at:at + P]
 
-        def job_wx(pool, tag, c):
-            pt = pool.tile([P, 3, P], BF16, name="pt_wx", tag=tag)
-            ts = [tr(pt[:, i, :], wx[:, c, i, :], ident_b) for i in range(3)]
-            return ts, lambda eng: copy_on(eng, wx_t[:, c, :, :], pt[:])
+        def wih_pairs(pt, n):
+            return pt[:, 0:n * P].bitcast(BF16).rearrange("p (i u r) -> p r i u", u=P, r=2)
+
+        def job_ia(pool, tag, c):
+            wit = wt[c]["wit"]
+            pt = pool.tile([P, NB], F32, name="pt_i", tag=tag)
+            ts = [tr(pt[:, i * P:(i + 1) * P], wih_words(c, i), ident_f) for i in range(4)]
+            return ts, lambda eng: copy_on(eng, wit[:, :, 0:4, :], wih_pairs(pt, 4))
+
+        def job_ib(pool, tag, c):
+            wit = wt[c]["wit"]
+            pt = pool.tile([P, NB], F32, name="pt_i", tag=tag)
+            px = pt[:, 2 * P:2 * P + 192].bitcast(BF16).rearrange("p (i u) -> p i u", u=P)
+            ts = [tr(pt[:, i * P:(i + 1) * P], wih_words(c, 4 + i), ident_f) for i in range(2)]
+            ts.extend([tr(px[:, i, :], wx[:, c, i, :], ident_b) for i in range(3)])
+
+            def out_copies(eng):
+                copy_on(eng, wit[:, :, 4:6, :], wih_pairs(pt, 2))
+                copy_on(eng, wx_t[:, c, :, :], px)
+            return ts, out_copies
 
         def job_w(pool, tag, c, ge):
             wn_w = wt[c]["wn"][:].bitcast(F32)
@@ -234,6 +249,12 @@ def tile_wavernncell_pa_kernel(tc, x, feat, aux1, h, w_ih, w_hh, b_ih, b_hh, out
             ps = ut[s]["gi_r"]
             return [mm(ps[:], wit[:, r, e, :], fa_t[:, r, bs], r == 0, r == 1) for r in range(2)]
 
+        def x0_r(s):
+            c, bh, e = unit_of(s)
+            ra = work.tile([P, NB], F32, name="ra", tag="ra", bufs=6)
+            ut[s]["ra"] = ra
+            stt(ra[:], xb_v[:, bh * NB:(bh + 1) * NB, 0], wt[c]["w01"][:, 0, e, 0:1], ut[s]["gi_r"][:], ALU.mult, ALU.add)
+
         def pe_mx(s):
             c, bh, e = unit_of(s)
             wc, ws = wt[c]["wc"], wt[c]["ws"]
@@ -254,47 +275,32 @@ def tile_wavernncell_pa_kernel(tc, x, feat, aux1, h, w_ih, w_hh, b_ih, b_hh, out
             gz = acc.tile([P, 2, 256], F32, name="gz", tag="acc")
             gn = acc.tile([P, 2, 256], F32, name="gn", tag="acc")
             bt[b] = {"gz": gz, "gn": gn}
-            seq = []
-            for k in range(2):
-                t = 4 * bh + 2 * j + k
-                cols = slice(t * P, (t + 1) * P)
-                loc = slice((2 * j + k) * P, (2 * j + k + 1) * P)
-                wz = [wit[:, r, 2:4, :].rearrange("p e u -> p (e u)") for r in range(2)]
-                wn = [wit[:, r, 4:6, :].rearrange("p e u -> p (e u)") for r in range(2)]
-                wnx = wx_t[:, c, 0:2, :].rearrange("p e u -> p (e u)")
-                tz = [tacc(gz[:, k, e * P:(e + 1) * P], ut[2 * m + e]["zc"][:, loc], e == 1) for e in range(2)]
-                tn = [tacc(gn[:, k, e * P:(e + 1) * P], ut[2 * m + e]["rq"][:, loc], e == 1) for e in range(2)]
-                z = [mm(gz[:, k, :], fa_t[:, r, cols], wz[r], r == 0, False) for r in range(2)]
-                z.append(mm(gz[:, k, 0:P], x_t[:, cols], wx_t[:, c, 2, :], False, False))
-                n = [mm(gn[:, k, :], fa_t[:, r, cols], wn[r], r == 0, False) for r in range(2)]
-                n.append(mm(gn[:, k, :], x_t[:, cols], wnx, False, False))
-                seq.append((z, n, tz, tn))
-            return seq
+            ops = []
+            for G, ps, src, nx in ((1, gz, "zc", 1), (2, gn, "rq", 2)):
+                for k in range(2):
+                    t = 4 * bh + 2 * j + k
+                    cols = slice(t * P, (t + 1) * P)
+                    loc = slice((2 * j + k) * P, (2 * j + k + 1) * P)
+                    for r in range(2):
+                        w = wit[:, r, 2 * G:2 * G + 2, :].rearrange("p e u -> p (e u)")
+                        ops.append((mm(ps[:, k, :], fa_t[:, r, cols], w, r == 0, False), True))
+                    wx_g = wx_t[:, c, 0:2, :] if G == 2 else wx_t[:, c, 2:3, :]
+                    ops.append((mm(ps[:, k, 0:nx * P], x_t[:, cols], wx_g.rearrange("p e u -> p (e u)"), False, False),
+                                G == 2))
+                    for e in range(2):
+                        ops.append((tacc(ps[:, k, e * P:(e + 1) * P], ut[2 * m + e][src][:, loc], e == 1), False))
+            return ops
 
         def plain(k, prep_ts):
-            r = []
-            if k + 1 < NSTEP:
-                begin_unit(k + 1)
-                r = pe_gi_r(k + 1)
-            if k < 2:
-                weave(r, prep_ts)
-                return
-            (z, n, tz, tn), (z2, n2, tz2, tn2) = pe_b(k - 2)
-            ms = [z[0], n[0], z[1], n[1], z[2], n[2]]
-            for i in range(2):
-                if r:
-                    ms.append(r[i])
-                ms.append(tz[i])
-            ms.extend([z2[0], tn[0], z2[1], tn[1], n2[0], z2[2], n2[1], tz2[0], n2[2], tz2[1], tn2[0], tn2[1]])
-            weave(ms, prep_ts)
+            weave(pe_b(k - 2) if k >= 2 else [], prep_ts)
 
-        def acts_b(b):
-            z = work.tile([P, 2, 256], F32, name="zt", tag="zt", bufs=3)
-            n = work.tile([P, 2, 256], F32, name="nt", tag="nt", bufs=4)
-            nc.scalar.activation(out=z[:], in_=bt[b]["gz"][:], func=AF.Sigmoid, scale=-1.0)
-            nc.scalar.activation(out=n[:], in_=bt[b]["gn"][:], func=AF.Tanh)
-            bt[b]["z"] = z
-            bt[b]["n"] = n
+        def sig_b(b):
+            bt[b]["z"] = work.tile([P, 2, 256], F32, name="zt", tag="zt", bufs=3)
+            nc.scalar.activation(out=bt[b]["z"][:], in_=bt[b]["gz"][:], func=AF.Sigmoid, scale=-1.0)
+
+        def tanh_b(b):
+            bt[b]["n"] = work.tile([P, 2, 256], F32, name="nt", tag="nt", bufs=4)
+            nc.scalar.activation(out=bt[b]["n"][:], in_=bt[b]["gn"][:], func=AF.Tanh)
 
         def h_of(b):
             m, j = b // 2, b % 2
@@ -320,9 +326,8 @@ def tile_wavernncell_pa_kernel(tc, x, feat, aux1, h, w_ih, w_hh, b_ih, b_hh, out
                 return []
             w = [("w", c, ge) for ge in range(6)]
             if c == 1:
-                return [[("h", t, 0) for t in range(4, 8)], w[0:4], w[4:6] + [("ia", c, 0)],
-                        [("ib", c, 0), ("wx", c, 0)]][k % 4]
-            return [w[0:2], w[2:4] + [("ia", c, 0)], w[4:6], [("ib", c, 0), ("wx", c, 0)]][k % 4]
+                return [[("h", t, 0) for t in range(4, 8)], w[0:4], w[4:6], [("ia", c, 0), ("ib", c, 0)]][k % 4]
+            return [w[0:2], w[2:4], w[4:6], [("ia", c, 0), ("ib", c, 0)]][k % 4]
 
         def make_job(d, pool, tag):
             kind, c, i = d
@@ -333,10 +338,8 @@ def tile_wavernncell_pa_kernel(tc, x, feat, aux1, h, w_ih, w_hh, b_ih, b_hh, out
             if kind == "h":
                 return job_h(pool, tag, c)
             if kind == "ia":
-                return job_i(pool, tag, c, 0, 4)
-            if kind == "ib":
-                return job_i(pool, tag, c, 4, 6)
-            return job_wx(pool, tag, c)
+                return job_ia(pool, tag, c)
+            return job_ib(pool, tag, c)
 
         def quants(k):
             for kind, c, i in prep_jobs(k - 1) if k > 0 else []:
@@ -348,12 +351,15 @@ def tile_wavernncell_pa_kernel(tc, x, feat, aux1, h, w_ih, w_hh, b_ih, b_hh, out
 
         def step(k):
             main = k < NSTEP
+            b = k - 2
+            if 0 <= b - 1 < NSTEP:
+                tanh_b(b - 1)
+                sub_mul_b(b - 1, "pool" if b < NSTEP else "dve")
             if main:
                 pe_mx(k)
             if main and k % 4 == 2 and k // 4 + 1 < 4:
                 small_w(k // 4 + 1)
-            jobs = [make_job(d, tp, "tp") for d in prep_jobs(k)[0:2]]
-            late = prep_jobs(k)[2:]
+            jobs = [make_job(d, tp if i < 2 else acc, "tp" if i < 2 else "acc") for i, d in enumerate(prep_jobs(k))]
             ts = []
             for j in jobs:
                 ts.extend(j[0])
@@ -372,36 +378,38 @@ def tile_wavernncell_pa_kernel(tc, x, feat, aux1, h, w_ih, w_hh, b_ih, b_hh, out
                     a1 = work.tile([P, NB], F32, name="a1", tag="a1", bufs=2)
                     nc.scalar.activation(out=a1[:], in_=x1, func=AF.Identity, bias=b_z[:, i:i + 1],
                                          scale=w01[:, 1, 1, 1:2])
-                ra = work.tile([P, NB], F32, name="ra", tag="ra", bufs=2)
+                ra = u["ra"]
                 rb = work.tile([P, NB], F32, name="rb", tag="rb", bufs=2)
                 rq = work.tile([P, NB], F32, name="rq", tag="rq", bufs=5)
                 u["rq"] = rq
-                stt(ra[:], x0, w01[:, 0, e, 0:1], u["gi_r"][:], ALU.mult, ALU.add)
-                if k >= 4:
-                    out_b(k - 4)
                 stt(rb[:], x1, w01[:, 0, e, 1:2], u["gh0"][:], ALU.mult, ALU.add)
                 if e == 1:
                     stt(zc[:], x0, w01[:, 1, 1, 0:1], u["gh1"][:], ALU.mult, ALU.add)
                 tt("dve", ra[:], ra[:], rb[:], ALU.add)
-                quants(k)
                 nc.scalar.activation(out=ra[:], in_=ra[:], func=AF.Sigmoid, bias=b_r[:, i:i + 1], scale=1.0)
-                stt(rq[:], u["gh2"][:], b_t[:, 40 + i:41 + i], ra[:], ALU.add, ALU.mult)
                 if e == 1:
                     tt("dve", zc[:], zc[:], a1[:], ALU.add)
+                elif k >= 4:
+                    out_b(k - 4)
+                stt(rq[:], u["gh2"][:], b_t[:, 40 + i:41 + i], ra[:], ALU.add, ALU.mult)
+                if e == 1 and k >= 4:
+                    out_b(k - 4)
+                quants(k)
             elif k - 4 < NSTEP:
                 out_b(k - 4)
-            if k < NSTEP + 2:
+            if b < NSTEP:
                 plain(k, ts)
-            for j in jobs:
-                j[1]("act")
-            for d in late:
-                j = make_job(d, tp, "tp")
-                for t in j[0]:
-                    t()
-                j[1]("act")
-            if 2 <= k < NSTEP + 2:
-                acts_b(k - 2)
-                sub_mul_b(k - 2, "pool" if k < NSTEP + 1 else "dve")
+            for i, j in enumerate(jobs):
+                if i == 1 and 0 <= b < NSTEP:
+                    sig_b(b)
+                j[1]("dve" if k < 3 and i % 2 == 1 else "act")
+            if len(jobs) < 2 and 0 <= b < NSTEP:
+                sig_b(b)
+            if k + 1 in range(NHEAD, NSTEP):
+                begin_unit(k + 1)
+                for r in pe_gi_r(k + 1):
+                    r()
+                x0_r(k + 1)
 
         count = [0]
 
@@ -413,34 +421,47 @@ def tile_wavernncell_pa_kernel(tc, x, feat, aux1, h, w_ih, w_hh, b_ih, b_hh, out
                 t()
             job[1]("act" if i % 2 == 0 else "dve")
 
+        def early_r(s, i):
+            if i == 0:
+                begin_unit(s)
+            pe_gi_r(s)[i]()
+            if i == 1:
+                x0_r(s)
+
         begin_w(0)
-        for t in range(4):
-            run_job(job_h, t)
-        run_job(job_w, 0, 0)
-        run_job(job_w, 0, 1)
-        quant_h(0, 0)
-        quant_h(1, 0)
         run_job(job_fa, 0)
         run_job(job_fa, 1)
-        quant_w(0, 0)
         small_w(0)
-        run_job(job_i, 0, 0, 4)
+        run_job(job_ia, 0)
+        early_r(0, 0)
+        early_r(0, 1)
+        early_r(1, 0)
+        early_r(1, 1)
+        run_job(job_h, 0)
+        early_r(2, 0)
+        run_job(job_h, 1)
+        early_r(2, 1)
+        run_job(job_h, 2)
+        run_job(job_h, 3)
+        early_r(3, 0)
+        run_job(job_w, 0, 0)
+        quant_h(0, 0)
+        quant_h(1, 0)
+        run_job(job_w, 0, 1)
+        early_r(3, 1)
         run_job(job_bias)
         nc.vector.tensor_tensor(out=b_r[:], in0=b_t[:, 0:8], in1=b_t[:, 24:32], op=ALU.add)
         nc.vector.tensor_tensor(out=b_z[:], in0=b_t[:, 8:16], in1=b_t[:, 32:40], op=ALU.add)
         nc.vector.tensor_copy(out=wx[:, :, 0:2, ONE], in_=b_t[:, 16:24].rearrange("p (c e) -> p c e", e=2))
-        begin_unit(0)
-        for m in pe_gi_r(0):
-            m()
         run_job(job_w, 0, 2)
+        quant_w(0, 0)
         run_job(job_w, 0, 3)
         run_job(job_x)
         quant_w(0, 1)
         run_job(job_w, 0, 4)
         run_job(job_w, 0, 5)
-        run_job(job_i, 0, 4, 6)
         quant_w(0, 2)
-        run_job(job_wx, 0)
+        run_job(job_ib, 0)
 
         for k in range(NSTEP + 4):
             if k % 4 == 0 and k < NSTEP and k // 4 + 2 < 4:

@@ -23,23 +23,6 @@ WROW = 800
 FLOPS = 2 * B * 3 * H * (H + IN)
 
 
-def weave(ops, ts):
-    gaps = sum(1 for op in ops[:-1] if op[1])
-    seen = 0
-    done = 0
-    for i, op in enumerate(ops):
-        op[0]()
-        if op[1] and i < len(ops) - 1:
-            seen += 1
-            hi = (seen * len(ts) + gaps - 1) // gaps
-            while done < hi:
-                ts[done]()
-                done += 1
-    while done < len(ts):
-        ts[done]()
-        done += 1
-
-
 def tile_wavernncell_pa_kernel(tc, x, feat, aux1, h, w_ih, w_hh, b_ih, b_hh, out):
     nc = tc.nc
     with ExitStack() as ctx:
@@ -275,24 +258,35 @@ def tile_wavernncell_pa_kernel(tc, x, feat, aux1, h, w_ih, w_hh, b_ih, b_hh, out
             gz = acc.tile([P, 2, 256], F32, name="gz", tag="acc")
             gn = acc.tile([P, 2, 256], F32, name="gn", tag="acc")
             bt[b] = {"gz": gz, "gn": gn}
-            ops = []
-            for G, ps, src, nx in ((1, gz, "zc", 1), (2, gn, "rq", 2)):
-                for k in range(2):
+            halves = []
+            for k in range(2):
+                ms, ts = [], []
+                for G, ps, src, nx in ((1, gz, "zc", 1), (2, gn, "rq", 2)):
                     t = 4 * bh + 2 * j + k
                     cols = slice(t * P, (t + 1) * P)
                     loc = slice((2 * j + k) * P, (2 * j + k + 1) * P)
                     for r in range(2):
                         w = wit[:, r, 2 * G:2 * G + 2, :].rearrange("p e u -> p (e u)")
-                        ops.append((mm(ps[:, k, :], fa_t[:, r, cols], w, r == 0, False), True))
+                        ms.append(mm(ps[:, k, :], fa_t[:, r, cols], w, r == 0, False))
                     wx_g = wx_t[:, c, 0:2, :] if G == 2 else wx_t[:, c, 2:3, :]
-                    ops.append((mm(ps[:, k, 0:nx * P], x_t[:, cols], wx_g.rearrange("p e u -> p (e u)"), False, False),
-                                G == 2))
+                    ms.append(mm(ps[:, k, 0:nx * P], x_t[:, cols], wx_g.rearrange("p e u -> p (e u)"), False, False))
                     for e in range(2):
-                        ops.append((tacc(ps[:, k, e * P:(e + 1) * P], ut[2 * m + e][src][:, loc], e == 1), False))
-            return ops
+                        ts.append(tacc(ps[:, k, e * P:(e + 1) * P], ut[2 * m + e][src][:, loc], e == 1))
+                halves.append((ms, ts))
+            return halves
 
         def plain(k, prep_ts):
-            weave(pe_b(k - 2) if k >= 2 else [], prep_ts)
+            at = 0
+            for ms, ts in pe_b(k - 2) if k >= 2 else []:
+                for op in ms:
+                    op()
+                for op in prep_ts[at:at + len(prep_ts) // 2]:
+                    op()
+                at += len(prep_ts) // 2
+                for op in ts:
+                    op()
+            for op in prep_ts[at:]:
+                op()
 
         def sig_b(b):
             bt[b]["z"] = work.tile([P, 2, 256], F32, name="zt", tag="zt", bufs=3)

@@ -74,7 +74,7 @@ def tile_wavernncell_pa_kernel(tc, x, feat, aux1, h, w_ih, w_hh, b_ih, b_hh, out
                 nc.sync.dma_start(out=wt[c]["win"][:, e, 0:3 * IN].rearrange("p (G k) -> p G k", k=IN), in_=wih_v[c, e])
 
         def new_w(c):
-            win = wpool.tile([P, 2, WROW], BF16, name="win", tag="win")
+            win = wpool.tile([P, 2, WROW], BF16, name="win", tag="win", bufs=3)
             wn = wpool.tile([P, 3, 2, H], BF16, name="wn", tag="wn")
             wt[c] = {"win": win, "wn": wn}
 
@@ -223,7 +223,7 @@ def tile_wavernncell_pa_kernel(tc, x, feat, aux1, h, w_ih, w_hh, b_ih, b_hh, out
             return lambda: nc.tensor.matmul(dst, lhsT=src, rhs=ident_f[:], is_transpose=True, start=False, stop=stop)
 
         def begin_unit(s):
-            ut[s] = {"gi_r": acc.tile([P, NB], F32, name="gi_r", tag="acc")}
+            ut.setdefault(s, {})["gi_r"] = acc.tile([P, NB], F32, name="gi_r", tag="acc")
 
         def pe_gi_r(s):
             c, bh, e = unit_of(s)
@@ -232,11 +232,59 @@ def tile_wavernncell_pa_kernel(tc, x, feat, aux1, h, w_ih, w_hh, b_ih, b_hh, out
             ps = ut[s]["gi_r"]
             return [mm(ps[:], wit[:, r, e, :], fa_t[:, r, bs], r == 0, r == 1) for r in range(2)]
 
+        def x_of(s, col):
+            bh = unit_of(s)[1]
+            return xb_v[:, bh * NB:(bh + 1) * NB, col]
+
+        def tile_at(s):
+            return 2 * unit_of(s)[0] + unit_of(s)[2]
+
         def x0_r(s):
             c, bh, e = unit_of(s)
             ra = work.tile([P, NB], F32, name="ra", tag="ra", bufs=6)
             ut[s]["ra"] = ra
-            stt(ra[:], xb_v[:, bh * NB:(bh + 1) * NB, 0], wt[c]["w01"][:, 0, e, 0:1], ut[s]["gi_r"][:], ALU.mult, ALU.add)
+            stt(ra[:], x_of(s, 0), wt[c]["w01"][:, 0, e, 0:1], ut[s]["gi_r"][:], ALU.mult, ALU.add)
+
+        def x1_r(s):
+            c, bh, e = unit_of(s)
+            ra = ut[s]["ra"]
+            stt(ra[:], x_of(s, 1), wt[c]["w01"][:, 0, e, 1:2], ra[:], ALU.mult, ALU.add)
+
+        def add_r(s):
+            ra = ut[s]["ra"]
+            tt("dve", ra[:], ut[s]["gh0"][:], ra[:], ALU.add)
+
+        def sig_r(s):
+            i = tile_at(s)
+            ra = ut[s]["ra"]
+            nc.scalar.activation(out=ra[:], in_=ra[:], func=AF.Sigmoid, bias=b_r[:, i:i + 1], scale=1.0)
+
+        def mul_n(s):
+            i = tile_at(s)
+            rq = work.tile([P, NB], F32, name="rq", tag="rq", bufs=5)
+            ut[s]["rq"] = rq
+            stt(rq[:], ut[s]["gh2"][:], b_t[:, 40 + i:41 + i], ut[s]["ra"][:], ALU.add, ALU.mult)
+
+        def even_z(s):
+            i = tile_at(s)
+            zc = work.tile([P, NB], F32, name="zc", tag="zc", bufs=5)
+            ut[s]["zc"] = zc
+            nc.scalar.activation(out=zc[:], in_=ut[s]["gh1"][:], func=AF.Identity, bias=b_z[:, i:i + 1], scale=1.0)
+
+        def x1_z(s):
+            i = tile_at(s)
+            zc = work.tile([P, NB], F32, name="zc", tag="zc", bufs=5)
+            ut.setdefault(s, {})["zc"] = zc
+            nc.scalar.activation(out=zc[:], in_=x_of(s, 1), func=AF.Identity, bias=b_z[:, i:i + 1],
+                                 scale=wt[unit_of(s)[0]]["w01"][:, 1, 1, 1:2])
+
+        def x0_z(s):
+            zc = ut[s]["zc"]
+            stt(zc[:], x_of(s, 0), wt[unit_of(s)[0]]["w01"][:, 1, 1, 0:1], zc[:], ALU.mult, ALU.add)
+
+        def add_z(s):
+            zc = ut[s]["zc"]
+            tt("dve", zc[:], ut[s]["gh1"][:], zc[:], ALU.add)
 
         def pe_mx(s):
             c, bh, e = unit_of(s)
@@ -260,33 +308,21 @@ def tile_wavernncell_pa_kernel(tc, x, feat, aux1, h, w_ih, w_hh, b_ih, b_hh, out
             bt[b] = {"gz": gz, "gn": gn}
             halves = []
             for k in range(2):
+                t = 4 * bh + 2 * j + k
+                cols = slice(t * P, (t + 1) * P)
+                loc = slice((2 * j + k) * P, (2 * j + k + 1) * P)
                 ms, ts = [], []
-                for G, ps, src, nx in ((1, gz, "zc", 1), (2, gn, "rq", 2)):
-                    t = 4 * bh + 2 * j + k
-                    cols = slice(t * P, (t + 1) * P)
-                    loc = slice((2 * j + k) * P, (2 * j + k + 1) * P)
+                for G, ps, src in ((1, gz, "zc"), (2, gn, "rq")):
                     for r in range(2):
                         w = wit[:, r, 2 * G:2 * G + 2, :].rearrange("p e u -> p (e u)")
                         ms.append(mm(ps[:, k, :], fa_t[:, r, cols], w, r == 0, False))
-                    wx_g = wx_t[:, c, 0:2, :] if G == 2 else wx_t[:, c, 2:3, :]
-                    ms.append(mm(ps[:, k, 0:nx * P], x_t[:, cols], wx_g.rearrange("p e u -> p (e u)"), False, False))
+                    if G == 1:
+                        ms.append(mm(ps[:, k, 0:P], x_t[:, cols], wx_t[:, c, 2, :], False, False))
                     for e in range(2):
-                        ts.append(tacc(ps[:, k, e * P:(e + 1) * P], ut[2 * m + e][src][:, loc], e == 1))
-                halves.append((ms, ts))
+                        ts.append(tacc(ps[:, k, e * P:(e + 1) * P], ut[2 * m + e][src][:, loc], G == 1 and e == 1))
+                last = mm(gn[:, k, :], x_t[:, cols], wx_t[:, c, 0:2, :].rearrange("p e u -> p (e u)"), False, True)
+                halves.append((ms, ts, last))
             return halves
-
-        def plain(k, prep_ts):
-            at = 0
-            for ms, ts in pe_b(k - 2) if k >= 2 else []:
-                for op in ms:
-                    op()
-                for op in prep_ts[at:at + len(prep_ts) // 2]:
-                    op()
-                at += len(prep_ts) // 2
-                for op in ts:
-                    op()
-            for op in prep_ts[at:]:
-                op()
 
         def sig_b(b):
             bt[b]["z"] = work.tile([P, 2, 256], F32, name="zt", tag="zt", bufs=3)
@@ -302,11 +338,11 @@ def tile_wavernncell_pa_kernel(tc, x, feat, aux1, h, w_ih, w_hh, b_ih, b_hh, out
             t = 4 * bh + 2 * j
             return hn[:, t:t + 2, 256 * c:256 * (c + 1)], out_v[:, t:t + 2, 256 * c:256 * (c + 1)]
 
-        def sub_mul_b(b, eng):
-            hv = h_of(b)[0]
-            n, z = bt[b]["n"], bt[b]["z"]
-            tt(eng, n[:], n[:], hv, ALU.subtract)
-            tt(eng, n[:], z[:], n[:], ALU.mult)
+        def sub_b(b, eng):
+            tt(eng, bt[b]["n"][:], bt[b]["n"][:], h_of(b)[0], ALU.subtract)
+
+        def mul_b(b, eng):
+            tt(eng, bt[b]["n"][:], bt[b]["z"][:], bt[b]["n"][:], ALU.mult)
 
         def out_b(b):
             hv, ov = h_of(b)
@@ -315,13 +351,14 @@ def tile_wavernncell_pa_kernel(tc, x, feat, aux1, h, w_ih, w_hh, b_ih, b_hh, out
             nc.sync.dma_start(out=ov, in_=o[:])
 
         def prep_jobs(k):
-            c = k // 4 + 1
-            if k >= NSTEP or c > 3:
-                return []
-            w = [("w", c, ge) for ge in range(6)]
-            if c == 1:
-                return [[("h", t, 0) for t in range(4, 8)], w[0:4], w[4:6], [("ia", c, 0), ("ib", c, 0)]][k % 4]
-            return [w[0:2], w[2:4], w[4:6], [("ia", c, 0), ("ib", c, 0)]][k % 4]
+            w = [("w", 1, ge) for ge in range(6)]
+            if k < 3:
+                return [[("h", t, 0) for t in range(4, 8)], w[0:4] + [("ia", 1, 0)], w[4:6]][k]
+            c, i = (k + 5) // 4, (k + 1) % 4
+            if c > 3:
+                return [("ib", 3, 0)] if k == 11 else []
+            w = [("ib", c - 1, 0)] + [("w", c, ge) for ge in range(6)] + [("ia", c, 0)]
+            return w[2 * i:2 * i + 2]
 
         def make_job(d, pool, tag):
             kind, c, i = d
@@ -346,65 +383,65 @@ def tile_wavernncell_pa_kernel(tc, x, feat, aux1, h, w_ih, w_hh, b_ih, b_hh, out
         def step(k):
             main = k < NSTEP
             b = k - 2
-            if 0 <= b - 1 < NSTEP:
+            if 1 <= b <= NSTEP:
                 tanh_b(b - 1)
-                sub_mul_b(b - 1, "pool" if b < NSTEP else "dve")
+                eng = "pool" if b < NSTEP else "dve"
+                sub_b(b - 1, eng)
+                sig_b(b - 1)
+                mul_b(b - 1, eng)
             if main:
                 pe_mx(k)
-            if main and k % 4 == 2 and k // 4 + 1 < 4:
-                small_w(k // 4 + 1)
-            jobs = [make_job(d, tp if i < 2 else acc, "tp" if i < 2 else "acc") for i, d in enumerate(prep_jobs(k))]
-            ts = []
-            for j in jobs:
-                ts.extend(j[0])
+            if k in (2, 5, 9):
+                small_w({2: 1, 5: 2, 9: 3}[k])
             if main:
-                u = ut[k]
-                c, bh, e = unit_of(k)
-                i = 2 * c + e
-                w01 = wt[c]["w01"]
-                bs = slice(bh * NB, (bh + 1) * NB)
-                x0, x1 = xb_v[:, bs, 0], xb_v[:, bs, 1]
-                zc = work.tile([P, NB], F32, name="zc", tag="zc", bufs=5)
-                u["zc"] = zc
-                if e == 0:
-                    nc.scalar.activation(out=zc[:], in_=u["gh1"][:], func=AF.Identity, bias=b_z[:, i:i + 1], scale=1.0)
-                else:
-                    a1 = work.tile([P, NB], F32, name="a1", tag="a1", bufs=2)
-                    nc.scalar.activation(out=a1[:], in_=x1, func=AF.Identity, bias=b_z[:, i:i + 1],
-                                         scale=w01[:, 1, 1, 1:2])
-                ra = u["ra"]
-                rb = work.tile([P, NB], F32, name="rb", tag="rb", bufs=2)
-                rq = work.tile([P, NB], F32, name="rq", tag="rq", bufs=5)
-                u["rq"] = rq
-                stt(rb[:], x1, w01[:, 0, e, 1:2], u["gh0"][:], ALU.mult, ALU.add)
-                if e == 1:
-                    stt(zc[:], x0, w01[:, 1, 1, 0:1], u["gh1"][:], ALU.mult, ALU.add)
-                tt("dve", ra[:], ra[:], rb[:], ALU.add)
-                nc.scalar.activation(out=ra[:], in_=ra[:], func=AF.Sigmoid, bias=b_r[:, i:i + 1], scale=1.0)
-                if e == 1:
-                    tt("dve", zc[:], zc[:], a1[:], ALU.add)
-                elif k >= 4:
-                    out_b(k - 4)
-                stt(rq[:], u["gh2"][:], b_t[:, 40 + i:41 + i], ra[:], ALU.add, ALU.mult)
-                if e == 1 and k >= 4:
-                    out_b(k - 4)
+                if k % 2 == 0:
+                    even_z(k)
+                add_r(k)
+                sig_r(k)
+                if k % 2 == 1:
+                    add_z(k)
+                if k == 1:
+                    quants(k)
+                if NHEAD <= k + 1 < NSTEP:
+                    begin_unit(k + 1)
+                    for r in pe_gi_r(k + 1):
+                        r()
+                    x0_r(k + 1)
+                mul_n(k)
+            todo = prep_jobs(k)
+            if k < 2:
+                jobs = [make_job(d, tp if i < 2 else acc, "tp" if i < 2 else "acc") for i, d in enumerate(todo)]
+                for job in jobs:
+                    for op in job[0]:
+                        op()
+                for i, job in enumerate(jobs):
+                    job[1]("dve" if i % 2 == 1 else "act")
+            halves = pe_b(b) if 0 <= b < NSTEP else []
+            for i in range(len(halves)):
+                ms, ts, last = halves[i]
+                for op in ms:
+                    op()
+                jobs = [make_job(d, tp, "tp") for d in todo[i::2]]
+                for job in jobs:
+                    for op in job[0]:
+                        op()
+                for op in ts:
+                    op()
+                last()
+                for job in jobs:
+                    job[1]("dve" if k < 3 and i == 1 else "act")
+                if i == 0 and k % 2 == 0 and k + 1 < NSTEP:
+                    x1_z(k + 1)
+            if k == 0:
+                x1_z(1)
+            if main and k != 1:
                 quants(k)
-            elif k - 4 < NSTEP:
+            if k + 1 < NSTEP:
+                x1_r(k + 1)
+                if k % 2 == 0:
+                    x0_z(k + 1)
+            if 0 <= k - 4 < NSTEP:
                 out_b(k - 4)
-            if b < NSTEP:
-                plain(k, ts)
-            for i, j in enumerate(jobs):
-                if i == 1 and 0 <= b < NSTEP:
-                    sig_b(b)
-                j[1]("dve" if k < 3 and i % 2 == 1 else "act")
-            if len(jobs) < 2 and 0 <= b < NSTEP:
-                sig_b(b)
-            if k + 1 in range(NHEAD, NSTEP):
-                begin_unit(k + 1)
-                for r in pe_gi_r(k + 1):
-                    r()
-                x0_r(k + 1)
-
         count = [0]
 
         def run_job(make, *args):
@@ -456,11 +493,13 @@ def tile_wavernncell_pa_kernel(tc, x, feat, aux1, h, w_ih, w_hh, b_ih, b_hh, out
         run_job(job_w, 0, 5)
         quant_w(0, 2)
         run_job(job_ib, 0)
+        x1_r(0)
 
         for k in range(NSTEP + 4):
-            if k % 4 == 0 and k < NSTEP and k // 4 + 2 < 4:
-                new_w(k // 4 + 2)
+            if k in (0, 3):
+                c = 2 if k == 0 else 3
+                new_w(c)
                 for G in range(3):
-                    load_whh(k // 4 + 2, G)
-                load_wih(k // 4 + 2)
+                    load_whh(c, G)
+                load_wih(c)
             step(k)

@@ -18,6 +18,7 @@ IN = 258
 NB = 512
 NSTEP = 16
 NHEAD = 4
+NTAIL = 3
 ONE = 16
 WROW = 800
 FLOPS = 2 * B * 3 * H * (H + IN)
@@ -136,10 +137,26 @@ def tile_wavernncell_pa_kernel(tc, x, feat, aux1, h, w_ih, w_hh, b_ih, b_hh, out
             pt = pool.tile([P, P], BF16, name="pt_b", tag=tag)
             return [tr(pt[:], bn[:], ident_b)], lambda eng: copy_on(eng, b_t[:], pt[:, 0:48])
 
+        perm = {}
+
+        def permute(eng, kind, c, i):
+            if kind == "h":
+                src = hn_w[:, c, :]
+            else:
+                src = wt[c]["wn"][:].rearrange("p G e k -> p (G e k)").bitcast(F32)[:, 512 * i:512 * (i + 1)]
+            pm = work.tile([P, 4, P], F32, name="pm", tag="pm", bufs=6)
+            copy_on(eng, pm[:].rearrange("p (g u) q -> p g u q", g=2), src.rearrange("p (g q u) -> p g u q", g=2, u=2))
+            perm[(kind, c, i)] = pm
+
+        def words(kind, c, i, row):
+            if (kind, c, i) in perm:
+                return [perm[(kind, c, i)][:, j, :] for j in range(4)]
+            return [row[:, 256 * g + u:256 * (g + 1):2] for g in range(2) for u in range(2)]
+
         def job_h(pool, tag, t):
             pt = pool.tile([P, 4, P], F32, name="pt_h", tag=tag)
-            ts = [tr(pt[:, 2 * g + u, :], hn_w[:, t, 256 * g + u:256 * (g + 1):2], ident_f)
-                  for g in range(2) for u in range(2)]
+            src = words("h", t, 0, hn_w[:, t, :])
+            ts = [tr(pt[:, i, :], src[i], ident_f) for i in range(4)]
             return ts, lambda eng: copy_on(eng, hg_w[:, :, t * P:(t + 1) * P, :],
                                            pt[:].rearrange("p (g u) b -> p g b u", g=2))
 
@@ -185,10 +202,9 @@ def tile_wavernncell_pa_kernel(tc, x, feat, aux1, h, w_ih, w_hh, b_ih, b_hh, out
         def job_w(pool, tag, c, ge):
             wn_w = wt[c]["wn"][:].bitcast(F32)
             wg_w = wt[c]["wg"][:].bitcast(F32)
-            G, e = ge // 2, ge % 2
             pt = pool.tile([P, 4, P], F32, name="pt_w", tag=tag)
-            ts = [tr(pt[:, 2 * g + u, :], wn_w[:, G, e, 256 * g + u:256 * (g + 1):2], ident_f)
-                  for g in range(2) for u in range(2)]
+            src = words("w", c, ge, wn_w[:, ge // 2, ge % 2, :])
+            ts = [tr(pt[:, i, :], src[i], ident_f) for i in range(4)]
             return ts, lambda eng: copy_on(eng, wg_w[:, ge, :, :, :],
                                            pt[:].rearrange("p (g u) q -> p g q u", g=2))
 
@@ -385,7 +401,7 @@ def tile_wavernncell_pa_kernel(tc, x, feat, aux1, h, w_ih, w_hh, b_ih, b_hh, out
             b = k - 2
             if 1 <= b <= NSTEP:
                 tanh_b(b - 1)
-                eng = "pool" if b < NSTEP else "dve"
+                eng = "pool" if b - 1 < NSTEP - NTAIL else "dve"
                 sub_b(b - 1, eng)
                 sig_b(b - 1)
                 mul_b(b - 1, eng)
@@ -419,13 +435,15 @@ def tile_wavernncell_pa_kernel(tc, x, feat, aux1, h, w_ih, w_hh, b_ih, b_hh, out
             halves = pe_b(b) if 0 <= b < NSTEP else []
             for i in range(len(halves)):
                 ms, ts, last = halves[i]
-                for op in ms:
-                    op()
                 jobs = [make_job(d, tp, "tp") for d in todo[i::2]]
+                prep = []
                 for job in jobs:
-                    for op in job[0]:
-                        op()
-                for op in ts:
+                    prep.extend(job[0])
+                for j, op in enumerate(ms):
+                    op()
+                    if j != 2 and prep:
+                        prep.pop(0)()
+                for op in prep + ts:
                     op()
                 last()
                 for job in jobs:
@@ -478,8 +496,12 @@ def tile_wavernncell_pa_kernel(tc, x, feat, aux1, h, w_ih, w_hh, b_ih, b_hh, out
         run_job(job_w, 0, 0)
         quant_h(0, 0)
         quant_h(1, 0)
+        permute("act", "w", 0, 2)
+        permute("act", "w", 0, 3)
         run_job(job_w, 0, 1)
         early_r(3, 1)
+        permute("act", "w", 0, 4)
+        permute("act", "w", 0, 5)
         run_job(job_bias)
         nc.vector.tensor_tensor(out=b_r[:], in0=b_t[:, 0:8], in1=b_t[:, 24:32], op=ALU.add)
         nc.vector.tensor_tensor(out=b_z[:], in0=b_t[:, 8:16], in1=b_t[:, 32:40], op=ALU.add)

@@ -55,8 +55,8 @@ def tile_wavernncell_pa_kernel(tc, x, feat, aux1, h, w_ih, w_hh, b_ih, b_hh, out
         xb = const.tile([P, 2 * B], BF16, name="xb")
         hn = const.tile([P, 8, H], BF16, name="hn")
         hg = const.tile([P, 2, B, 4], BF16, name="hg", align_bytes=64)
-        hc = const.tile([P, 2, B], U32, name="hc", align_bytes=64)
-        hs = const.tile([P, 2, B], U8, name="hs", align_bytes=64)
+        hc = const.tile([P, 2, B], U32, name="hc", align_bytes=256)
+        hs = const.tile([P, 2, B], U8, name="hs", align_bytes=256)
         wx = const.tile([P, 4, 3, P], BF16, name="wx")
         wx_t = const.tile([P, 4, 3, P], BF16, name="wx_t")
         b_t = const.tile([P, 48], F32, name="b_t")
@@ -91,10 +91,10 @@ def tile_wavernncell_pa_kernel(tc, x, feat, aux1, h, w_ih, w_hh, b_ih, b_hh, out
         nc.sync.dma_start(out=fan[:, :, 0:P], in_=feat_v)
         nc.sync.dma_start(out=fan[:, :, P:2 * P], in_=aux_v)
         load_wih(0)
-        for k in range(2):
-            nc.sync.dma_start(out=hn[:, 2 * k:2 * k + 2, :], in_=h_v[:, 2 * k:2 * k + 2, :])
-        load_whh(0, 0)
+        nc.sync.dma_start(out=hn[:, 0:2, :], in_=h_v[:, 0:2, :])
         nc.sync.dma_start(out=xb[:], in_=x.rearrange("b c -> (b c)").partition_broadcast(P))
+        nc.sync.dma_start(out=hn[:, 2:4, :], in_=h_v[:, 2:4, :])
+        load_whh(0, 0)
         with nc.allow_non_contiguous_dma(reason="x: four bytes a piece"):
             nc.scalar.dma_start(out=xn[:, :, 0:2], in_=x_v)
         nc.scalar.dma_start(out=bn[0:24, :], in_=bih_v)
@@ -165,8 +165,8 @@ def tile_wavernncell_pa_kernel(tc, x, feat, aux1, h, w_ih, w_hh, b_ih, b_hh, out
             w["w01"] = wpool.tile([P, 3, 2, 2], F32, name="w01", tag="w01", bufs=3)
             w["wit"] = wpool.tile([P, 2, 6, P], BF16, name="wit", tag="wit", bufs=3)
             w["wg"] = wpool.tile([P, 6, 2, P, 4], BF16, name="wg", tag="wg", align_bytes=64)
-            w["wc"] = wpool.tile([P, 6, 2, P], U32, name="wc", tag="wc", align_bytes=64)
-            w["ws"] = wpool.tile([P, 6, 2, P], U8, name="ws", tag="ws", align_bytes=64)
+            w["wc"] = wpool.tile([P, 6, 2, P], U32, name="wc", tag="wc", align_bytes=256)
+            w["ws"] = wpool.tile([P, 6, 2, P], U8, name="ws", tag="ws", align_bytes=256)
 
         def small_w(c):
             win = wt[c]["win"][:, :, 0:3 * IN].rearrange("p e (G k) -> p G e k", k=IN)
@@ -322,6 +322,7 @@ def tile_wavernncell_pa_kernel(tc, x, feat, aux1, h, w_ih, w_hh, b_ih, b_hh, out
             gz = acc.tile([P, 2, 256], F32, name="gz", tag="acc")
             gn = acc.tile([P, 2, 256], F32, name="gn", tag="acc")
             bt[b] = {"gz": gz, "gn": gn}
+            begin_b(b)
             halves = []
             for k in range(2):
                 t = 4 * bh + 2 * j + k
@@ -340,31 +341,33 @@ def tile_wavernncell_pa_kernel(tc, x, feat, aux1, h, w_ih, w_hh, b_ih, b_hh, out
                 halves.append((ms, ts, last))
             return halves
 
-        def sig_b(b):
-            bt[b]["z"] = work.tile([P, 2, 256], F32, name="zt", tag="zt", bufs=3)
-            nc.scalar.activation(out=bt[b]["z"][:], in_=bt[b]["gz"][:], func=AF.Sigmoid, scale=-1.0)
+        def begin_b(b):
+            for name in ("z", "n", "o"):
+                bt[b][name] = work.tile([P, 2, 256], F32, name=name + "t", tag=name + "t", bufs=4)
 
-        def tanh_b(b):
-            bt[b]["n"] = work.tile([P, 2, 256], F32, name="nt", tag="nt", bufs=4)
-            nc.scalar.activation(out=bt[b]["n"][:], in_=bt[b]["gn"][:], func=AF.Tanh)
+        def sig_b(b, lo, hi):
+            nc.scalar.activation(out=bt[b]["z"][:, lo:hi, :], in_=bt[b]["gz"][:, lo:hi, :], func=AF.Sigmoid, scale=-1.0)
 
-        def h_of(b):
+        def tanh_b(b, lo, hi):
+            nc.scalar.activation(out=bt[b]["n"][:, lo:hi, :], in_=bt[b]["gn"][:, lo:hi, :], func=AF.Tanh)
+
+        def place_of(b, lo, hi):
             m, j = b // 2, b % 2
             c, bh = m // 2, m % 2
             t = 4 * bh + 2 * j
-            return hn[:, t:t + 2, 256 * c:256 * (c + 1)], out_v[:, t:t + 2, 256 * c:256 * (c + 1)]
+            return slice(t + lo, t + hi), slice(256 * c, 256 * (c + 1))
 
-        def sub_b(b, eng):
-            tt(eng, bt[b]["n"][:], bt[b]["n"][:], h_of(b)[0], ALU.subtract)
+        def sub_b(b, lo, hi, eng):
+            ts, js = place_of(b, lo, hi)
+            tt(eng, bt[b]["n"][:, lo:hi, :], bt[b]["n"][:, lo:hi, :], hn[:, ts, js], ALU.subtract)
 
-        def mul_b(b, eng):
-            tt(eng, bt[b]["n"][:], bt[b]["z"][:], bt[b]["n"][:], ALU.mult)
+        def mul_b(b, lo, hi, eng):
+            tt(eng, bt[b]["n"][:, lo:hi, :], bt[b]["z"][:, lo:hi, :], bt[b]["n"][:, lo:hi, :], ALU.mult)
 
-        def out_b(b):
-            hv, ov = h_of(b)
-            o = work.tile([P, 2, 256], F32, name="ot", tag="ot", bufs=3)
-            tt("dve", o[:], bt[b]["n"][:], hv, ALU.add)
-            nc.sync.dma_start(out=ov, in_=o[:])
+        def out_b(b, lo, hi):
+            ts, js = place_of(b, lo, hi)
+            tt("dve", bt[b]["o"][:, lo:hi, :], bt[b]["n"][:, lo:hi, :], hn[:, ts, js], ALU.add)
+            nc.sync.dma_start(out=out_v[:, ts, js], in_=bt[b]["o"][:, lo:hi, :])
 
         def prep_jobs(k):
             w = [("w", 1, ge) for ge in range(6)]
@@ -400,11 +403,12 @@ def tile_wavernncell_pa_kernel(tc, x, feat, aux1, h, w_ih, w_hh, b_ih, b_hh, out
             main = k < NSTEP
             b = k - 2
             if 1 <= b <= NSTEP:
-                tanh_b(b - 1)
-                eng = "pool" if b - 1 < NSTEP - NTAIL else "dve"
-                sub_b(b - 1, eng)
-                sig_b(b - 1)
-                mul_b(b - 1, eng)
+                tanh_b(b - 1, 0, 2)
+                if b - 1 < NSTEP - NTAIL:
+                    sub_b(b - 1, 0, 2, "pool")
+                sig_b(b - 1, 0, 2)
+                if b - 1 < NSTEP - NTAIL:
+                    mul_b(b - 1, 0, 2, "pool")
             if main:
                 pe_mx(k)
             if k in (2, 5, 9):
@@ -431,7 +435,7 @@ def tile_wavernncell_pa_kernel(tc, x, feat, aux1, h, w_ih, w_hh, b_ih, b_hh, out
                     for op in job[0]:
                         op()
                 for i, job in enumerate(jobs):
-                    job[1]("dve" if i % 2 == 1 else "act")
+                    job[1]("dve" if i == 2 - k else "act")
             halves = pe_b(b) if 0 <= b < NSTEP else []
             for i in range(len(halves)):
                 ms, ts, last = halves[i]
@@ -458,8 +462,8 @@ def tile_wavernncell_pa_kernel(tc, x, feat, aux1, h, w_ih, w_hh, b_ih, b_hh, out
                 x1_r(k + 1)
                 if k % 2 == 0:
                     x0_z(k + 1)
-            if 0 <= k - 4 < NSTEP:
-                out_b(k - 4)
+            if 0 <= k - 4 < NSTEP - NTAIL:
+                out_b(k - 4, 0, 2)
         count = [0]
 
         def run_job(make, *args):
@@ -468,7 +472,7 @@ def tile_wavernncell_pa_kernel(tc, x, feat, aux1, h, w_ih, w_hh, b_ih, b_hh, out
             job = make(tp, "tp", *args) if i % 4 == 3 else make(acc, "acc", *args)
             for t in job[0]:
                 t()
-            job[1]("act" if i % 2 == 0 else "dve")
+            job[1]("act" if i % 2 == 0 or i > 14 else "dve")
 
         def early_r(s, i):
             if i == 0:
@@ -486,6 +490,8 @@ def tile_wavernncell_pa_kernel(tc, x, feat, aux1, h, w_ih, w_hh, b_ih, b_hh, out
         early_r(0, 1)
         early_r(1, 0)
         early_r(1, 1)
+        permute("act", "h", 2, 0)
+        permute("act", "h", 3, 0)
         run_job(job_h, 0)
         early_r(2, 0)
         run_job(job_h, 1)
@@ -510,14 +516,14 @@ def tile_wavernncell_pa_kernel(tc, x, feat, aux1, h, w_ih, w_hh, b_ih, b_hh, out
         quant_w(0, 0)
         run_job(job_w, 0, 3)
         run_job(job_x)
+        x1_r(0)
         quant_w(0, 1)
         run_job(job_w, 0, 4)
         run_job(job_w, 0, 5)
         quant_w(0, 2)
         run_job(job_ib, 0)
-        x1_r(0)
 
-        for k in range(NSTEP + 4):
+        for k in range(NSTEP + 3):
             if k in (0, 3):
                 c = 2 if k == 0 else 3
                 new_w(c)
@@ -525,3 +531,15 @@ def tile_wavernncell_pa_kernel(tc, x, feat, aux1, h, w_ih, w_hh, b_ih, b_hh, out
                     load_whh(c, G)
                 load_wih(c)
             step(k)
+        p, q = NSTEP - 2, NSTEP - 1
+        sub_b(p - 1, 0, 2, "dve")
+        mul_b(p - 1, 0, 2, "dve")
+        out_b(p - 1, 0, 2)
+        sub_b(p, 0, 2, "dve")
+        mul_b(p, 0, 2, "dve")
+        sub_b(q, 0, 2, "dve")
+        out_b(p, 0, 2)
+        mul_b(q, 0, 1, "dve")
+        mul_b(q, 1, 2, "dve")
+        out_b(q, 0, 1)
+        out_b(q, 1, 2)

from contextlib import ExitStack

import concourse.mybir as mybir
from concourse.masks import make_identity

F32 = mybir.dt.float32
BF16 = mybir.dt.bfloat16
U32 = mybir.dt.uint32
U8 = mybir.dt.uint8
FP8X4 = mybir.dt.float8_e4m3fn_x4
ALU = mybir.AluOpType
AF = mybir.ActivationFunctionType

P = 128
B = 1024
H = 1024
IN = 258
NB = 512
NSTEP = 16
NHEAD = 4
NTAIL = 3
ONE = 16
WROW = 800
FLOPS = 2 * B * 3 * H * (H + IN)


def tile_wavernncell_pa_kernel(tc, x, feat, aux1, h, w_ih, w_hh, b_ih, b_hh, out):
    nc = tc.nc
    with ExitStack() as ctx:
        ctx.enter_context(tc.manual_schedule())
        const = ctx.enter_context(tc.tile_pool(name="const", bufs=1))
        wpool = ctx.enter_context(tc.tile_pool(name="wpool", bufs=2))
        work = ctx.enter_context(tc.tile_pool(name="work", bufs=2))
        acc = ctx.enter_context(tc.psum_pool(name="acc", bufs=6))
        tp = ctx.enter_context(tc.psum_pool(name="tp", bufs=2))

        x_v = x.rearrange("(t p) c -> p t c", p=P)
        feat_v = feat.rearrange("(t p) k -> p t k", p=P)
        aux_v = aux1.rearrange("(t p) k -> p t k", p=P)
        h_v = h.rearrange("(t p) k -> p t k", p=P)
        out_v = out.rearrange("(t p) j -> p t j", p=P)
        wih_v = w_ih.rearrange("(G c e p) k -> c e p G k", G=3, c=4, e=2, p=P)
        whh_v = w_hh.rearrange("(G c e p) k -> c G p e k", G=3, c=4, e=2, p=P)
        bih_v = b_ih.rearrange("(m u) -> m u", u=P)
        bhh_v = b_hh.rearrange("(m u) -> m u", u=P)

        ident_f = const.tile([P, P], F32, name="ident_f")
        ident_b = const.tile([P, P], BF16, name="ident_b")
        warm = const.tile([P, 1], F32, name="warm")
        fan = const.tile([P, 8, 2 * P], BF16, name="fan")
        xn = const.tile([P, 8, P], BF16, name="xn")
        bn = const.tile([P, P], BF16, name="bn")
        fa_t = const.tile([P, 2, B], BF16, name="fa_t")
        x_t = const.tile([P, B], BF16, name="x_t")
        xb = const.tile([P, 2 * B], BF16, name="xb")
        hn = const.tile([P, 8, H], BF16, name="hn")
        hg = const.tile([P, 2, B, 4], BF16, name="hg", align_bytes=64)
        hc = const.tile([P, 2, B], U32, name="hc", align_bytes=256)
        hs = const.tile([P, 2, B], U8, name="hs", align_bytes=256)
        wx = const.tile([P, 4, 3, P], BF16, name="wx")
        wx_t = const.tile([P, 4, 3, P], BF16, name="wx_t")
        b_t = const.tile([P, 48], F32, name="b_t")
        b_r = const.tile([P, 8], F32, name="b_r")
        b_z = const.tile([P, 8], F32, name="b_z")

        wt = {}
        ut = {}
        bt = {}

        def load_whh(c, G):
            nc.sync.dma_start(out=wt[c]["wn"][:, G, :, :], in_=whh_v[c, G])

        def load_wih(c):
            for e in range(2):
                nc.sync.dma_start(out=wt[c]["win"][:, e, 0:3 * IN].rearrange("p (G k) -> p G k", k=IN), in_=wih_v[c, e])

        def new_w(c):
            win = wpool.tile([P, 2, WROW], BF16, name="win", tag="win", bufs=3)
            wn = wpool.tile([P, 3, 2, H], BF16, name="wn", tag="wn")
            wt[c] = {"win": win, "wn": wn}

        nc.vector.memset(warm[:], 0.0)
        nc.vector.memset(xn[:], 0.0)
        nc.vector.memset(xn[:, :, ONE:ONE + 1], 1.0)
        nc.vector.memset(bn[:], 0.0)
        nc.vector.memset(wx[:], 0.0)
        make_identity(nc, ident_f[:])
        make_identity(nc, ident_b[:])
        new_w(0)
        new_w(1)
        nc.sync.dma_start(out=fan[:, :, 0:P], in_=feat_v)
        nc.sync.dma_start(out=fan[:, :, P:2 * P], in_=aux_v)
        load_wih(0)
        nc.sync.dma_start(out=hn[:, 0:2, :], in_=h_v[:, 0:2, :])
        nc.sync.dma_start(out=xb[:], in_=x.rearrange("b c -> (b c)").partition_broadcast(P))
        nc.sync.dma_start(out=hn[:, 2:4, :], in_=h_v[:, 2:4, :])
        load_whh(0, 0)
        with nc.allow_non_contiguous_dma(reason="x: four bytes a piece"):
            nc.scalar.dma_start(out=xn[:, :, 0:2], in_=x_v)
        nc.scalar.dma_start(out=bn[0:24, :], in_=bih_v)
        nc.scalar.dma_start(out=bn[24:48, :], in_=bhh_v)
        load_whh(0, 1)
        load_whh(0, 2)
        for k in range(2, 4):
            nc.sync.dma_start(out=hn[:, 2 * k:2 * k + 2, :], in_=h_v[:, 2 * k:2 * k + 2, :])
        for G in range(3):
            load_whh(1, G)
        load_wih(1)
        nc.scalar.activation(out=warm[:], in_=warm[:], func=AF.Sigmoid)

        xb_v = xb[:].rearrange("p (b c) -> p b c", c=2)
        hn_w = hn[:].bitcast(F32)
        hg_w = hg[:].bitcast(F32)
        fan_w = fan[:].bitcast(F32)

        def copy_on(eng, dst, src):
            if eng == "act":
                nc.scalar.copy(out=dst, in_=src)
            else:
                nc.vector.tensor_copy(out=dst, in_=src)

        def tr(dst, src, ident):
            return lambda: nc.tensor.transpose(dst, src, ident[:])

        def job_fa(pool, tag, i):
            pt = pool.tile([P, 4, P], F32, name="pt_f", tag=tag)
            ts = [tr(pt[:, t, :], fan_w[:, 4 * i + t, :], ident_f) for t in range(4)]
            src = pt[:].rearrange("p t b -> p (t b)").bitcast(BF16).rearrange("p (b r) -> p r b", r=2)
            return ts, lambda eng: copy_on(eng, fa_t[:, :, NB * i:NB * (i + 1)], src)

        def job_x(pool, tag):
            pt = pool.tile([P, 8, P], BF16, name="pt_x", tag=tag)
            ts = [tr(pt[:, t, :], xn[:, t, :], ident_b) for t in range(8)]
            return ts, lambda eng: copy_on(eng, x_t[:], pt[:].rearrange("p t b -> p (t b)"))

        def job_bias(pool, tag):
            pt = pool.tile([P, P], BF16, name="pt_b", tag=tag)
            return [tr(pt[:], bn[:], ident_b)], lambda eng: copy_on(eng, b_t[:], pt[:, 0:48])

        perm = {}

        def permute(eng, kind, c, i):
            if kind == "h":
                src = hn_w[:, c, :]
            else:
                src = wt[c]["wn"][:].rearrange("p G e k -> p (G e k)").bitcast(F32)[:, 512 * i:512 * (i + 1)]
            pm = work.tile([P, 4, P], F32, name="pm", tag="pm", bufs=6)
            copy_on(eng, pm[:].rearrange("p (g u) q -> p g u q", g=2), src.rearrange("p (g q u) -> p g u q", g=2, u=2))
            perm[(kind, c, i)] = pm

        def words(kind, c, i, row):
            if (kind, c, i) in perm:
                return [perm[(kind, c, i)][:, j, :] for j in range(4)]
            return [row[:, 256 * g + u:256 * (g + 1):2] for g in range(2) for u in range(2)]

        def job_h(pool, tag, t):
            pt = pool.tile([P, 4, P], F32, name="pt_h", tag=tag)
            src = words("h", t, 0, hn_w[:, t, :])
            ts = [tr(pt[:, i, :], src[i], ident_f) for i in range(4)]
            return ts, lambda eng: copy_on(eng, hg_w[:, :, t * P:(t + 1) * P, :],
                                           pt[:].rearrange("p (g u) b -> p g b u", g=2))

        def begin_w(c):
            w = wt[c]
            w["w01"] = wpool.tile([P, 3, 2, 2], F32, name="w01", tag="w01", bufs=3)
            w["wit"] = wpool.tile([P, 2, 6, P], BF16, name="wit", tag="wit", bufs=3)
            w["wg"] = wpool.tile([P, 6, 2, P, 4], BF16, name="wg", tag="wg", align_bytes=64)
            w["wc"] = wpool.tile([P, 6, 2, P], U32, name="wc", tag="wc", align_bytes=256)
            w["ws"] = wpool.tile([P, 6, 2, P], U8, name="ws", tag="ws", align_bytes=256)

        def small_w(c):
            win = wt[c]["win"][:, :, 0:3 * IN].rearrange("p e (G k) -> p G e k", k=IN)
            nc.scalar.copy(out=wt[c]["w01"][:], in_=win[:, :, :, 256:258])
            nc.scalar.copy(out=wx[:, c, 0:2, 0:2], in_=win[:, 2, :, 256:258])
            nc.scalar.copy(out=wx[:, c, 2, 0:2], in_=win[:, 1, 0, 256:258])

        def wih_words(c, i):
            at = WROW // 2 * (i % 2) + 129 * (i // 2)
            return wt[c]["win"][:].rearrange("p e k -> p (e k)").bitcast(F32)[:, at:at + P]

        def wih_pairs(pt, n):
            return pt[:, 0:n * P].bitcast(BF16).rearrange("p (i u r) -> p r i u", u=P, r=2)

        def job_ia(pool, tag, c):
            wit = wt[c]["wit"]
            pt = pool.tile([P, NB], F32, name="pt_i", tag=tag)
            ts = [tr(pt[:, i * P:(i + 1) * P], wih_words(c, i), ident_f) for i in range(4)]
            return ts, lambda eng: copy_on(eng, wit[:, :, 0:4, :], wih_pairs(pt, 4))

        def job_ib(pool, tag, c):
            wit = wt[c]["wit"]
            pt = pool.tile([P, NB], F32, name="pt_i", tag=tag)
            px = pt[:, 2 * P:2 * P + 192].bitcast(BF16).rearrange("p (i u) -> p i u", u=P)
            ts = [tr(pt[:, i * P:(i + 1) * P], wih_words(c, 4 + i), ident_f) for i in range(2)]
            ts.extend([tr(px[:, i, :], wx[:, c, i, :], ident_b) for i in range(3)])

            def out_copies(eng):
                copy_on(eng, wit[:, :, 4:6, :], wih_pairs(pt, 2))
                copy_on(eng, wx_t[:, c, :, :], px)
            return ts, out_copies

        def job_w(pool, tag, c, ge):
            wn_w = wt[c]["wn"][:].bitcast(F32)
            wg_w = wt[c]["wg"][:].bitcast(F32)
            pt = pool.tile([P, 4, P], F32, name="pt_w", tag=tag)
            src = words("w", c, ge, wn_w[:, ge // 2, ge % 2, :])
            ts = [tr(pt[:, i, :], src[i], ident_f) for i in range(4)]
            return ts, lambda eng: copy_on(eng, wg_w[:, ge, :, :, :],
                                           pt[:].rearrange("p (g u) q -> p g q u", g=2))

        def quant_w(c, G):
            w = wt[c]
            nc.vector.quantize_mx(
                out=w["wc"][:, 2 * G:2 * G + 2, :, :].rearrange("p a g q -> p (a g q)").bitcast(FP8X4),
                scales=w["ws"][:, 2 * G:2 * G + 2, :, :].rearrange("p a g q -> p (a g q)"),
                in_=w["wg"][:, 2 * G:2 * G + 2, :, :, :].rearrange("p a g q t -> p (a g q t)"))

        def quant_h(g, bh):
            bs = slice(bh * NB, (bh + 1) * NB)
            nc.vector.quantize_mx(out=hc[:, g, bs].bitcast(FP8X4), scales=hs[:, g, bs],
                                  in_=hg[:, g, bs, :].rearrange("p b t -> p (b t)"))

        def stt(dst, in0, scalar, in1, op0, op1):
            nc.vector.scalar_tensor_tensor(out=dst, in0=in0, scalar=scalar, in1=in1, op0=op0, op1=op1)

        def tt(eng, dst, in0, in1, op):
            if eng == "dve":
                nc.vector.tensor_tensor(out=dst, in0=in0, in1=in1, op=op)
            else:
                nc.gpsimd.tensor_tensor(out=dst, in0=in0, in1=in1, op=op)

        def unit_of(s):
            return s // 4, (s // 2) % 2, s % 2

        def mm(ps, lhsT, rhs, start, stop):
            return lambda: nc.tensor.matmul(ps, lhsT=lhsT, rhs=rhs, start=start, stop=stop)

        def tacc(dst, src, stop):
            return lambda: nc.tensor.matmul(dst, lhsT=src, rhs=ident_f[:], is_transpose=True, start=False, stop=stop)

        def begin_unit(s):
            ut.setdefault(s, {})["gi_r"] = acc.tile([P, NB], F32, name="gi_r", tag="acc")

        def pe_gi_r(s):
            c, bh, e = unit_of(s)
            wit = wt[c]["wit"]
            bs = slice(bh * NB, (bh + 1) * NB)
            ps = ut[s]["gi_r"]
            return [mm(ps[:], wit[:, r, e, :], fa_t[:, r, bs], r == 0, r == 1) for r in range(2)]

        def x_of(s, col):
            bh = unit_of(s)[1]
            return xb_v[:, bh * NB:(bh + 1) * NB, col]

        def tile_at(s):
            return 2 * unit_of(s)[0] + unit_of(s)[2]

        def x0_r(s):
            c, bh, e = unit_of(s)
            ra = work.tile([P, NB], F32, name="ra", tag="ra", bufs=6)
            ut[s]["ra"] = ra
            stt(ra[:], x_of(s, 0), wt[c]["w01"][:, 0, e, 0:1], ut[s]["gi_r"][:], ALU.mult, ALU.add)

        def x1_r(s):
            c, bh, e = unit_of(s)
            ra = ut[s]["ra"]
            stt(ra[:], x_of(s, 1), wt[c]["w01"][:, 0, e, 1:2], ra[:], ALU.mult, ALU.add)

        def add_r(s):
            ra = ut[s]["ra"]
            tt("dve", ra[:], ut[s]["gh0"][:], ra[:], ALU.add)

        def sig_r(s):
            i = tile_at(s)
            ra = ut[s]["ra"]
            nc.scalar.activation(out=ra[:], in_=ra[:], func=AF.Sigmoid, bias=b_r[:, i:i + 1], scale=1.0)

        def mul_n(s):
            i = tile_at(s)
            rq = work.tile([P, NB], F32, name="rq", tag="rq", bufs=5)
            ut[s]["rq"] = rq
            stt(rq[:], ut[s]["gh2"][:], b_t[:, 40 + i:41 + i], ut[s]["ra"][:], ALU.add, ALU.mult)

        def even_z(s):
            i = tile_at(s)
            zc = work.tile([P, NB], F32, name="zc", tag="zc", bufs=5)
            ut[s]["zc"] = zc
            nc.scalar.activation(out=zc[:], in_=ut[s]["gh1"][:], func=AF.Identity, bias=b_z[:, i:i + 1], scale=1.0)

        def x1_z(s):
            i = tile_at(s)
            zc = work.tile([P, NB], F32, name="zc", tag="zc", bufs=5)
            ut.setdefault(s, {})["zc"] = zc
            nc.scalar.activation(out=zc[:], in_=x_of(s, 1), func=AF.Identity, bias=b_z[:, i:i + 1],
                                 scale=wt[unit_of(s)[0]]["w01"][:, 1, 1, 1:2])

        def x0_z(s):
            zc = ut[s]["zc"]
            stt(zc[:], x_of(s, 0), wt[unit_of(s)[0]]["w01"][:, 1, 1, 0:1], zc[:], ALU.mult, ALU.add)

        def add_z(s):
            zc = ut[s]["zc"]
            tt("dve", zc[:], ut[s]["gh1"][:], zc[:], ALU.add)

        def pe_mx(s):
            c, bh, e = unit_of(s)
            wc, ws = wt[c]["wc"], wt[c]["ws"]
            bs = slice(bh * NB, (bh + 1) * NB)
            for G in (0, 1, 2):
                ps = acc.tile([P, NB], F32, name="gh%d" % G, tag="acc")
                for kg in range(2):
                    nc.tensor.matmul_mx(ps[:], lhsT=wc[:, 2 * G + e, kg, :].bitcast(FP8X4),
                                        lhsT_scale=ws[:, 2 * G + e, kg, :],
                                        rhs=hc[:, kg, bs].bitcast(FP8X4), rhs_scale=hs[:, kg, bs],
                                        start=(kg == 0), stop=(kg == 1))
                ut[s]["gh%d" % G] = ps

        def pe_b(b):
            m, j = b // 2, b % 2
            c, bh = m // 2, m % 2
            wit = wt[c]["wit"]
            gz = acc.tile([P, 2, 256], F32, name="gz", tag="acc")
            gn = acc.tile([P, 2, 256], F32, name="gn", tag="acc")
            bt[b] = {"gz": gz, "gn": gn}
            begin_b(b)
            halves = []
            for k in range(2):
                t = 4 * bh + 2 * j + k
                cols = slice(t * P, (t + 1) * P)
                loc = slice((2 * j + k) * P, (2 * j + k + 1) * P)
                ms, ts = [], []
                for G, ps, src in ((1, gz, "zc"), (2, gn, "rq")):
                    for r in range(2):
                        w = wit[:, r, 2 * G:2 * G + 2, :].rearrange("p e u -> p (e u)")
                        ms.append(mm(ps[:, k, :], fa_t[:, r, cols], w, r == 0, False))
                    if G == 1:
                        ms.append(mm(ps[:, k, 0:P], x_t[:, cols], wx_t[:, c, 2, :], False, False))
                    for e in range(2):
                        ts.append(tacc(ps[:, k, e * P:(e + 1) * P], ut[2 * m + e][src][:, loc], G == 1 and e == 1))
                last = mm(gn[:, k, :], x_t[:, cols], wx_t[:, c, 0:2, :].rearrange("p e u -> p (e u)"), False, True)
                halves.append((ms, ts, last))
            return halves

        def begin_b(b):
            for name in ("z", "n", "o"):
                bt[b][name] = work.tile([P, 2, 256], F32, name=name + "t", tag=name + "t", bufs=4)

        def sig_b(b, lo, hi):
            nc.scalar.activation(out=bt[b]["z"][:, lo:hi, :], in_=bt[b]["gz"][:, lo:hi, :], func=AF.Sigmoid, scale=-1.0)

        def tanh_b(b, lo, hi):
            nc.scalar.activation(out=bt[b]["n"][:, lo:hi, :], in_=bt[b]["gn"][:, lo:hi, :], func=AF.Tanh)

        def place_of(b, lo, hi):
            m, j = b // 2, b % 2
            c, bh = m // 2, m % 2
            t = 4 * bh + 2 * j
            return slice(t + lo, t + hi), slice(256 * c, 256 * (c + 1))

        def sub_b(b, lo, hi, eng):
            ts, js = place_of(b, lo, hi)
            tt(eng, bt[b]["n"][:, lo:hi, :], bt[b]["n"][:, lo:hi, :], hn[:, ts, js], ALU.subtract)

        def mul_b(b, lo, hi, eng):
            tt(eng, bt[b]["n"][:, lo:hi, :], bt[b]["z"][:, lo:hi, :], bt[b]["n"][:, lo:hi, :], ALU.mult)

        def out_b(b, lo, hi):
            ts, js = place_of(b, lo, hi)
            tt("dve", bt[b]["o"][:, lo:hi, :], bt[b]["n"][:, lo:hi, :], hn[:, ts, js], ALU.add)
            nc.sync.dma_start(out=out_v[:, ts, js], in_=bt[b]["o"][:, lo:hi, :])

        def prep_jobs(k):
            w = [("w", 1, ge) for ge in range(6)]
            if k < 3:
                return [[("h", t, 0) for t in range(4, 8)], w[0:4] + [("ia", 1, 0)], w[4:6]][k]
            c, i = (k + 5) // 4, (k + 1) % 4
            if c > 3:
                return [("ib", 3, 0)] if k == 11 else []
            w = [("ib", c - 1, 0)] + [("w", c, ge) for ge in range(6)] + [("ia", c, 0)]
            return w[2 * i:2 * i + 2]

        def make_job(d, pool, tag):
            kind, c, i = d
            if kind == "w":
                if i == 0:
                    begin_w(c)
                return job_w(pool, tag, c, i)
            if kind == "h":
                return job_h(pool, tag, c)
            if kind == "ia":
                return job_ia(pool, tag, c)
            return job_ib(pool, tag, c)

        def quants(k):
            for kind, c, i in prep_jobs(k - 1) if k > 0 else []:
                if kind == "w" and i % 2 == 1:
                    quant_w(c, i // 2)
                if kind == "h" and c == 7:
                    quant_h(0, 1)
                    quant_h(1, 1)

        def step(k):
            main = k < NSTEP
            b = k - 2
            if 1 <= b <= NSTEP:
                tanh_b(b - 1, 0, 2)
                if b - 1 < NSTEP - NTAIL:
                    sub_b(b - 1, 0, 2, "pool")
                sig_b(b - 1, 0, 2)
                if b - 1 < NSTEP - NTAIL:
                    mul_b(b - 1, 0, 2, "pool")
            if main:
                pe_mx(k)
            if k in (2, 5, 9):
                small_w({2: 1, 5: 2, 9: 3}[k])
            if main:
                if k % 2 == 0:
                    even_z(k)
                add_r(k)
                sig_r(k)
                if k % 2 == 1:
                    add_z(k)
                if k == 1:
                    quants(k)
                if NHEAD <= k + 1 < NSTEP:
                    begin_unit(k + 1)
                    for r in pe_gi_r(k + 1):
                        r()
                    x0_r(k + 1)
                mul_n(k)
            todo = prep_jobs(k)
            if k < 2:
                jobs = [make_job(d, tp if i < 2 else acc, "tp" if i < 2 else "acc") for i, d in enumerate(todo)]
                for job in jobs:
                    for op in job[0]:
                        op()
                for i, job in enumerate(jobs):
                    job[1]("dve" if i == 2 - k else "act")
            halves = pe_b(b) if 0 <= b < NSTEP else []
            for i in range(len(halves)):
                ms, ts, last = halves[i]
                jobs = [make_job(d, tp, "tp") for d in todo[i::2]]
                prep = []
                for job in jobs:
                    prep.extend(job[0])
                for j, op in enumerate(ms):
                    op()
                    if j != 2 and prep:
                        prep.pop(0)()
                for op in prep + ts:
                    op()
                last()
                for job in jobs:
                    job[1]("dve" if k < 3 and i == 1 else "act")
                if i == 0 and k % 2 == 0 and k + 1 < NSTEP:
                    x1_z(k + 1)
            if k == 0:
                x1_z(1)
            if main and k != 1:
                quants(k)
            if k + 1 < NSTEP:
                x1_r(k + 1)
                if k % 2 == 0:
                    x0_z(k + 1)
            if 0 <= k - 4 < NSTEP - NTAIL:
                out_b(k - 4, 0, 2)
        count = [0]

        def run_job(make, *args):
            i = count[0]
            count[0] = i + 1
            job = make(tp, "tp", *args) if i % 4 == 3 else make(acc, "acc", *args)
            for t in job[0]:
                t()
            job[1]("act" if i % 2 == 0 or i > 14 else "dve")

        def early_r(s, i):
            if i == 0:
                begin_unit(s)
            pe_gi_r(s)[i]()
            if i == 1:
                x0_r(s)

        begin_w(0)
        run_job(job_fa, 0)
        run_job(job_fa, 1)
        small_w(0)
        run_job(job_ia, 0)
        early_r(0, 0)
        early_r(0, 1)
        early_r(1, 0)
        early_r(1, 1)
        permute("act", "h", 2, 0)
        permute("act", "h", 3, 0)
        run_job(job_h, 0)
        early_r(2, 0)
        run_job(job_h, 1)
        early_r(2, 1)
        run_job(job_h, 2)
        run_job(job_h, 3)
        early_r(3, 0)
        run_job(job_w, 0, 0)
        quant_h(0, 0)
        quant_h(1, 0)
        permute("act", "w", 0, 2)
        permute("act", "w", 0, 3)
        run_job(job_w, 0, 1)
        early_r(3, 1)
        permute("act", "w", 0, 4)
        permute("act", "w", 0, 5)
        run_job(job_bias)
        nc.vector.tensor_tensor(out=b_r[:], in0=b_t[:, 0:8], in1=b_t[:, 24:32], op=ALU.add)
        nc.vector.tensor_tensor(out=b_z[:], in0=b_t[:, 8:16], in1=b_t[:, 32:40], op=ALU.add)
        nc.vector.tensor_copy(out=wx[:, :, 0:2, ONE], in_=b_t[:, 16:24].rearrange("p (c e) -> p c e", e=2))
        run_job(job_w, 0, 2)
        quant_w(0, 0)
        run_job(job_w, 0, 3)
        run_job(job_x)
        x1_r(0)
        quant_w(0, 1)
        run_job(job_w, 0, 4)
        run_job(job_w, 0, 5)
        quant_w(0, 2)
        run_job(job_ib, 0)

        for k in range(NSTEP + 3):
            if k in (0, 3):
                c = 2 if k == 0 else 3
                new_w(c)
                for G in range(3):
                    load_whh(c, G)
                load_wih(c)
            step(k)
        p, q = NSTEP - 2, NSTEP - 1
        sub_b(p - 1, 0, 2, "dve")
        mul_b(p - 1, 0, 2, "dve")
        out_b(p - 1, 0, 2)
        sub_b(p, 0, 2, "dve")
        mul_b(p, 0, 2, "dve")
        sub_b(q, 0, 2, "dve")
        out_b(p, 0, 2)
        mul_b(q, 0, 1, "dve")
        mul_b(q, 1, 2, "dve")
        out_b(q, 0, 1)
        out_b(q, 1, 2)
